import numpy as np
import ml_dtypes


def mxq(x, axis, fmt="e4m3"):
    dtype, down = {"e4m3": (ml_dtypes.float8_e4m3fn, 7), "e5m2": (ml_dtypes.float8_e5m2, 14)}[fmt]
    v = np.moveaxis(np.asarray(x, np.float32).astype(ml_dtypes.bfloat16).astype(np.float64), axis, -1)
    blocks = v.reshape(v.shape[:-1] + (-1, 32))
    amax = np.abs(blocks).max(-1, keepdims=True)
    byte = np.maximum(np.where(amax > 0, np.frexp(amax)[1] - 1 + 127, 0) - down, 1)
    scale = np.exp2(byte - 127.0)
    codes = (blocks / scale).astype(np.float32).astype(dtype).astype(np.float64)
    return np.moveaxis((codes * scale).reshape(v.shape), -1, axis)


WIDE = False


def mx_kscale(k):
    if not WIDE:
        return np.ones(k)
    levels = np.array([10, -10, 5, -5, 0])
    a = np.random.permutation(np.resize(levels, k // 512 * 4)).reshape(k // 512, 4)
    idx = np.arange(k)
    return np.exp2(a[idx // 512, idx % 128 // 32])


BF16 = ml_dtypes.bfloat16


def bf(x):
    return np.asarray(x, np.float32).astype(BF16)


def f64(x):
    return np.asarray(x).astype(np.float64)


B, E, D1, D2, WS1, WS2, H, HID = 4, 512, 32, 32, 8, 8, 16, 2048
NW = (D1 // WS1) * (D2 // WS2)
S = WS1 * WS2
DH = E // H
EPS = 1e-5


def layernorm(v, g, b):
    mu = v.mean(-1, keepdims=True)
    var = v.var(-1, keepdims=True)
    return (v - mu) / np.sqrt(var + EPS) * g + b


def heads(t):
    return t.reshape(B, NW, S, H, DH).transpose(0, 1, 3, 2, 4)


def setup_inputs():
    n = np.random.standard_normal
    s = mx_kscale(E)
    c = 1.0 / np.sqrt(E)
    return {"x": bf(n((B, E, D1, D2))),
            "ln1_g": bf((1.0 + 0.1 * n(E)) * s), "ln1_b": bf(0.1 * n(E) * s),
            "Wq": bf(n((E, E)) * c / s[:, None]), "bq": bf(0.1 * n(E)),
            "Wk": bf(n((E, E)) * c / s[:, None]), "bk": bf(0.1 * n(E)),
            "Wv": bf(n((E, E)) * c / s[:, None]), "bv": bf(0.1 * n(E))}


def reference(x, ln1_g, ln1_b, Wq, bq, Wk, bk, Wv, bv):
    xt = f64(x).transpose(0, 2, 3, 1)
    xn = layernorm(xt, f64(ln1_g), f64(ln1_b))
    xn = np.roll(xn, (-WS1 // 2, -WS2 // 2), axis=(1, 2))
    xw = xn.reshape(B, D1 // WS1, WS1, D2 // WS2, WS2, E).transpose(0, 1, 3, 2, 4, 5).reshape(B, NW, S, E)
    xq = mxq(xw, 3, "e4m3")
    q = ((xq @ mxq(f64(Wq), 0, "e4m3")) + f64(bq)) * DH ** -0.5
    k = (xq @ mxq(f64(Wk), 0, "e4m3")) + f64(bk)
    v = (xq @ mxq(f64(Wv), 0, "e4m3")) + f64(bv)
    return heads(q), heads(k), heads(v)

@@ -1,0 +1,332 @@
+from contextlib import ExitStack
+
+import concourse.mybir as mybir
+from concourse.masks import make_identity
+
+BF16 = mybir.dt.bfloat16
+F32 = mybir.dt.float32
+U32 = mybir.dt.uint32
+U8 = mybir.dt.uint8
+FP8X4 = mybir.dt.float8_e4m3fn_x4
+ACT = mybir.ActivationFunctionType
+ALU = mybir.AluOpType
+
+P = 128
+PACK = 4
+BATCH = 4
+CHANNELS = P * PACK
+SIDE = 32
+TOKENS = SIDE * SIDE
+WIN = 8
+SHIFT = WIN // 2
+WIN_PER_SIDE = SIDE // WIN
+HEADS = 16
+HEAD_DIM = 32
+OUT_COLS = HEADS * HEAD_DIM
+EPS = 1e-5
+TILE_ROWS = P // SIDE
+TILES = TOKENS // P
+HALVES = WIN // TILE_ROWS
+SUM_COLS = 32
+UNITS = BATCH * WIN_PER_SIDE
+PASSES = 3 * WIN
+PASSES_PER_STEP = PASSES // WIN_PER_SIDE
+LAG = WIN_PER_SIDE + 1
+
+FLOPS = 2 * BATCH * TOKENS * CHANNELS * 3 * OUT_COLS
+
+
+def build_token_sort(nc, const):
+    ident_f32 = const.tile([P, P], F32)
+    make_identity(nc, ident_f32[:])
+    ident_rows = ident_f32[:].rearrange("p (r j) -> p r j", j=SIDE)
+    shifted = const.tile([P, TILE_ROWS, SIDE], F32)
+    nc.vector.tensor_copy(out=shifted[:, :, 0 : SIDE - SHIFT], in_=ident_rows[:, :, SHIFT:SIDE])
+    nc.vector.tensor_copy(out=shifted[:, :, SIDE - SHIFT : SIDE], in_=ident_rows[:, :, 0:SHIFT])
+    token_sort = const.tile([P, P], F32)
+    nc.vector.tensor_copy(
+        out=token_sort[:].rearrange("p (sj wj r) -> p sj wj r", sj=WIN, r=TILE_ROWS),
+        in_=shifted[:].rearrange("p r (wj sj) -> p sj wj r", sj=WIN),
+    )
+    return token_sort
+
+
+def tile_functatransformer_pa_t_kernel(
+    tc, x, ln1_g, ln1_b, Wq, bq, Wk, bk, Wv, bv, out_0, out_1, out_2
+):
+    nc = tc.nc
+    weights = (Wq, Wk, Wv)
+    biases = (bq, bk, bv)
+    outs = (out_0, out_1, out_2)
+    out_scales = (HEAD_DIM**-0.5, 1.0, 1.0)
+
+    with ExitStack() as ctx:
+        const = ctx.enter_context(tc.tile_pool(name="const", bufs=1))
+        images = ctx.enter_context(tc.tile_pool(name="images", bufs=BATCH))
+        wstage = ctx.enter_context(tc.tile_pool(name="wstage", bufs=3))
+        stats = ctx.enter_context(tc.tile_pool(name="stats", bufs=4))
+        norm = ctx.enter_context(tc.tile_pool(name="norm", bufs=4))
+        quant = ctx.enter_context(tc.tile_pool(name="quant", bufs=2))
+        results = ctx.enter_context(tc.tile_pool(name="results", bufs=4))
+        psum_x = ctx.enter_context(tc.psum_pool(name="psum_x", bufs=2))
+        psum_sum = ctx.enter_context(tc.psum_pool(name="psum_sum", bufs=1))
+        psum_y = ctx.enter_context(tc.psum_pool(name="psum_y", bufs=1))
+        psum_acc = ctx.enter_context(tc.psum_pool(name="psum_acc", bufs=3))
+        ctx.enter_context(tc.manual_schedule())
+
+        x_tiles = []
+        for b in range(BATCH):
+            x_sb = images.tile([P, PACK, TOKENS], BF16)
+            x_tiles.append(x_sb)
+
+        def load_image(b):
+            nc.sync.dma_start(
+                out=x_tiles[b][:], in_=x[b].rearrange("(p t) i j -> p t (i j)", t=PACK)
+            )
+
+        load_image(0)
+        gain_bf = const.tile([P, PACK], BF16)
+        shift_bf = const.tile([P, PACK], BF16)
+        nc.scalar.dma_start(out=gain_bf[:], in_=ln1_g.rearrange("(p t) -> p t", t=PACK))
+        nc.scalar.dma_start(out=shift_bf[:], in_=ln1_b.rearrange("(p t) -> p t", t=PACK))
+        w_raw = []
+        for o in range(3):
+            raw = wstage.tile([P, PACK, OUT_COLS], BF16)
+            nc.sync.dma_start(out=raw[:], in_=weights[o].rearrange("(p t) n -> p t n", t=PACK))
+            w_raw.append(raw)
+        for b in range(1, BATCH):
+            load_image(b)
+
+        eps = const.tile([P, 1], F32)
+        nc.vector.memset(eps[:], EPS)
+        warm = const.tile([P, 1], F32)
+        nc.scalar.activation(out=warm[:], in_=eps[:], func=ACT.Sqrt)
+        ones = const.tile([P, SUM_COLS], BF16)
+        nc.vector.memset(ones[:], 1.0)
+        ident_bf = const.tile([P, P], BF16)
+        make_identity(nc, ident_bf[:])
+        token_sort = build_token_sort(nc, const)
+        bias_bf = []
+        for o in range(3):
+            row = const.tile([P, OUT_COLS], BF16, name="bias_bf%d" % o)
+            nc.gpsimd.dma_start(out=row[:], in_=biases[o].partition_broadcast(P))
+            bias_bf.append(row)
+        gain = const.tile([P, PACK], F32)
+        shift = const.tile([P, PACK], F32)
+        nc.vector.tensor_copy(out=gain[:], in_=gain_bf[:])
+        nc.vector.tensor_copy(out=shift[:], in_=shift_bf[:])
+
+        w_codes = []
+        w_scales = []
+        bias_f32 = []
+
+        def prepare_weight(o):
+            w_grouped = wstage.tile([P, OUT_COLS, PACK], BF16, align_bytes=64)
+            nc.vector.tensor_copy(
+                out=w_grouped[:].rearrange("p (c i) t -> p c t i", i=4),
+                in_=w_raw[o][:].rearrange("p t (c i) -> p c t i", i=4),
+            )
+            row = const.tile([P, OUT_COLS], F32, name="bias_f32%d" % o)
+            nc.vector.tensor_scalar(
+                out=row[:], in0=bias_bf[o][:], scalar1=out_scales[o], scalar2=None, op0=ALU.mult
+            )
+            bias_f32.append(row)
+            codes = const.tile([P, OUT_COLS], U32, align_bytes=64, name="w_codes%d" % o)
+            scales = const.tile([P, OUT_COLS], U8, align_bytes=64, name="w_scales%d" % o)
+            nc.vector.quantize_mx(
+                out=codes[:].bitcast(FP8X4),
+                scales=scales[:],
+                in_=w_grouped[:].rearrange("p n t -> p (n t)"),
+            )
+            w_codes.append(codes)
+            w_scales.append(scales)
+
+        neg_mean_of = {}
+        x_t_of = {}
+        rstd_of = {}
+        neg_mean_rstd_of = {}
+        y_of = {}
+        y_t_of = {}
+        planes_of = {}
+        grouped_of = {}
+        x_codes_of = {}
+        x_scales_of = {}
+        result_of = {}
+
+        def first_token(u, half):
+            a = HALVES * (u % WIN_PER_SIDE) + half
+            return ((a + 1) % TILES) * P
+
+        def means(b):
+            sums = psum_sum.tile([P, TILES, SUM_COLS], F32)
+            for a in range(TILES):
+                first = first_token(a // HALVES, a % HALVES)
+                for t in range(PACK):
+                    nc.tensor.matmul(
+                        out=sums[:, a, :],
+                        lhsT=x_tiles[b][:, t, first : first + P],
+                        rhs=ones[:],
+                        start=(t == 0),
+                        stop=(t == PACK - 1),
+                    )
+            neg_mean = stats.tile([P, TILES], F32)
+            nc.vector.tensor_scalar(
+                out=neg_mean[:], in0=sums[:, :, 0], scalar1=-1.0 / CHANNELS, scalar2=None,
+                op0=ALU.mult,
+            )
+            neg_mean_of[b] = neg_mean
+
+        def tokens_to_partitions(u):
+            x_t = psum_x.tile([P, HALVES, PACK, P], BF16)
+            for half in range(HALVES):
+                first = first_token(u, half)
+                for t in range(PACK):
+                    nc.tensor.transpose(
+                        out=x_t[:, half, t, :],
+                        in_=x_tiles[u // WIN_PER_SIDE][:, t, first : first + P],
+                        identity=ident_bf[:],
+                    )
+            x_t_of[u] = x_t
+
+        def variance(u):
+            neg_mean = neg_mean_of[u // WIN_PER_SIDE]
+            slot = HALVES * (u % WIN_PER_SIDE)
+            sum_sq = stats.tile([P, HALVES], F32)
+            for half in range(HALVES):
+                squares = norm.tile([P, CHANNELS], BF16)
+                nc.scalar.activation(
+                    out=squares[:],
+                    in_=x_t_of[u][:, half].rearrange("p t c -> p (t c)"),
+                    func=ACT.Square,
+                    bias=neg_mean[:, slot + half : slot + half + 1],
+                    scale=1.0,
+                    accum_out=sum_sq[:, half : half + 1],
+                )
+            std = stats.tile([P, HALVES], F32)
+            nc.scalar.activation(
+                out=std[:], in_=sum_sq[:], func=ACT.Sqrt, bias=eps[:, 0:1], scale=1.0 / CHANNELS
+            )
+            rstd = stats.tile([P, HALVES], F32)
+            nc.vector.reciprocal(out=rstd[:], in_=std[:])
+            neg_mean_rstd = stats.tile([P, HALVES], F32)
+            nc.vector.tensor_tensor(
+                out=neg_mean_rstd[:], in0=neg_mean[:, slot : slot + HALVES], in1=rstd[:], op=ALU.mult
+            )
+            rstd_of[u] = rstd
+            neg_mean_rstd_of[u] = neg_mean_rstd
+
+        def normalise(u):
+            y_of[u] = []
+            for half in range(HALVES):
+                y = norm.tile([P, PACK, P], F32)
+                nc.scalar.activation(
+                    out=y[:].rearrange("p t c -> p (t c)"),
+                    in_=x_t_of[u][:, half].rearrange("p t c -> p (t c)"),
+                    func=ACT.Identity,
+                    bias=neg_mean_rstd_of[u][:, half : half + 1],
+                    scale=rstd_of[u][:, half : half + 1],
+                )
+                y_of[u].append(y)
+
+        def channels_to_partitions(u):
+            y_t_low = psum_y.tile([P, 2, HALVES, P], F32)
+            y_t_high = psum_y.tile([P, 2, HALVES, P], F32)
+            y_t_of[u] = (y_t_low, y_t_high)
+            for half in range(HALVES):
+                for t in range(PACK):
+                    nc.tensor.transpose(
+                        out=y_t_of[u][t // 2][:, t % 2, half, :],
+                        in_=y_of[u][half][:, t, :],
+                        identity=token_sort[:],
+                    )
+
+        def gain_and_shift(u):
+            planes = norm.tile([P, PACK, HALVES * P], BF16)
+            for t in range(PACK):
+                nc.scalar.activation(
+                    out=planes[:, t, :].rearrange(
+                        "p (g half r) -> p g half r", half=HALVES, r=TILE_ROWS
+                    ),
+                    in_=y_t_of[u][t // 2][:, t % 2].rearrange(
+                        "p half (g r) -> p g half r", r=TILE_ROWS
+                    ),
+                    func=ACT.Identity,
+                    bias=shift[:, t : t + 1],
+                    scale=gain[:, t : t + 1],
+                )
+            planes_of[u] = planes
+
+        def regroup(u):
+            b = u // WIN_PER_SIDE
+            wi = u % WIN_PER_SIDE
+            if wi == 0:
+                grouped = quant.tile([P, WIN, P, PACK], BF16, align_bytes=64)
+                grouped_of[b] = grouped
+            per_row = WIN_PER_SIDE * WIN
+            nc.vector.tensor_copy(
+                out=grouped_of[b][:, :, per_row * wi : per_row * (wi + 1), :].rearrange(
+                    "p sj (c i) t -> p sj c t i", i=4
+                ),
+                in_=planes_of[u][:].rearrange("p t (sj c i) -> p sj c t i", sj=WIN, i=4),
+            )
+            if wi == WIN_PER_SIDE - 1:
+                x_codes = quant.tile([P, WIN * P], U32, align_bytes=64)
+                x_scales = quant.tile([P, WIN * P], U8, align_bytes=64)
+                nc.vector.quantize_mx(
+                    out=x_codes[:].bitcast(FP8X4),
+                    scales=x_scales[:],
+                    in_=grouped_of[b][:].rearrange("p sj m t -> p (sj m t)"),
+                )
+                x_codes_of[b] = x_codes
+                x_scales_of[b] = x_scales
+
+        def project(b, o, sj):
+            if sj == 0:
+                result = results.tile([P, HEADS, WIN, HEAD_DIM], F32)
+                result_of[o] = result
+            acc = psum_acc.tile([P, OUT_COLS], F32)
+            nc.tensor.matmul_mx(
+                out=acc[:],
+                lhsT=x_codes_of[b][:, sj * P : (sj + 1) * P].bitcast(FP8X4),
+                lhsT_scale=x_scales_of[b][:, sj * P : (sj + 1) * P],
+                rhs=w_codes[o][:].bitcast(FP8X4),
+                rhs_scale=w_scales[o][:],
+                start=True,
+                stop=True,
+            )
+            nc.vector.scalar_tensor_tensor(
+                out=result_of[o][:, :, sj, :],
+                in0=acc[:].rearrange("p (h d) -> p h d", d=HEAD_DIM),
+                scalar=out_scales[o],
+                in1=bias_f32[o][:].rearrange("p (h d) -> p h d", d=HEAD_DIM),
+                op0=ALU.mult,
+                op1=ALU.add,
+            )
+            if sj == WIN - 1:
+                for h in range(HEADS):
+                    nc.sync.dma_start(
+                        out=outs[o][b, :, h].rearrange("w (si sj) d -> w si (sj d)", sj=WIN),
+                        in_=result_of[o][:, h].rearrange("p sj d -> p (sj d)"),
+                    )
+
+        for k in range(-1, UNITS + LAG):
+            if 0 <= k - 1 < UNITS:
+                channels_to_partitions(k - 1)
+            if 0 <= k + 1 < UNITS:
+                if (k + 1) % WIN_PER_SIDE == 0:
+                    means((k + 1) // WIN_PER_SIDE)
+                tokens_to_partitions(k + 1)
+            if 0 <= k < UNITS:
+                variance(k)
+            if 0 <= k - 1 < UNITS:
+                gain_and_shift(k - 1)
+            if 0 <= k < UNITS:
+                normalise(k)
+            if 0 <= k < 3:
+                prepare_weight(k)
+            if 0 <= k - LAG < UNITS:
+                for n in range(PASSES_PER_STEP):
+                    number = ((k - LAG) % WIN_PER_SIDE) * PASSES_PER_STEP + n
+                    project((k - LAG) // WIN_PER_SIDE, number // WIN, number % WIN)
+            if 0 <= k - 1 < UNITS:
+                regroup(k - 1)

@@ -263,11 +263,13 @@ def tile_functatransformer_pa_t_kernel(
                 grouped = quant.tile([P, WIN, P, PACK], BF16, align_bytes=64)
                 grouped_of[b] = grouped
             per_row = WIN_PER_SIDE * WIN
-            nc.vector.tensor_copy(
-                out=grouped_of[b][:, :, per_row * wi : per_row * (wi + 1), :].rearrange(
-                    "p sj (c i) t -> p sj c t i", i=4
-                ),
-                in_=planes_of[u][:].rearrange("p t (sj c i) -> p sj c t i", sj=WIN, i=4),
+            nc.gpsimd.tensor_scalar(
+                out=grouped_of[b][:, :, per_row * wi : per_row * (wi + 1), :],
+                in0=planes_of[u][:].rearrange("p t (sj c) -> p sj c t", sj=WIN),
+                scalar1=1.0,
+                scalar2=0.0,
+                op0=ALU.mult,
+                op1=ALU.add,
             )
             if wi == WIN_PER_SIDE - 1:
                 x_codes = quant.tile([P, WIN * P], U32, align_bytes=64)

@@ -157,24 +157,24 @@ def tile_functatransformer_pa_t_kernel(
             a = HALVES * (u % WIN_PER_SIDE) + half
             return ((a + 1) % TILES) * P
 
-        def means(b):
-            sums = psum_sum.tile([P, TILES, SUM_COLS], F32)
-            for a in range(TILES):
-                first = first_token(a // HALVES, a % HALVES)
+        def means(u):
+            sums = psum_sum.tile([P, HALVES, SUM_COLS], F32)
+            for half in range(HALVES):
+                first = first_token(u, half)
                 for t in range(PACK):
                     nc.tensor.matmul(
-                        out=sums[:, a, :],
-                        lhsT=x_tiles[b][:, t, first : first + P],
+                        out=sums[:, half, :],
+                        lhsT=x_tiles[u // WIN_PER_SIDE][:, t, first : first + P],
                         rhs=ones[:],
                         start=(t == 0),
                         stop=(t == PACK - 1),
                     )
-            neg_mean = stats.tile([P, TILES], F32)
+            neg_mean = stats.tile([P, HALVES], F32)
             nc.vector.tensor_scalar(
                 out=neg_mean[:], in0=sums[:, :, 0], scalar1=-1.0 / CHANNELS, scalar2=None,
                 op0=ALU.mult,
             )
-            neg_mean_of[b] = neg_mean
+            neg_mean_of[u] = neg_mean
 
         def tokens_to_partitions(u):
             x_t = psum_x.tile([P, HALVES, PACK, P], BF16)
@@ -189,8 +189,7 @@ def tile_functatransformer_pa_t_kernel(
             x_t_of[u] = x_t
 
         def variance(u):
-            neg_mean = neg_mean_of[u // WIN_PER_SIDE]
-            slot = HALVES * (u % WIN_PER_SIDE)
+            neg_mean = neg_mean_of[u]
             sum_sq = stats.tile([P, HALVES], F32)
             for half in range(HALVES):
                 squares = norm.tile([P, CHANNELS], BF16)
@@ -198,7 +197,7 @@ def tile_functatransformer_pa_t_kernel(
                     out=squares[:],
                     in_=x_t_of[u][:, half].rearrange("p t c -> p (t c)"),
                     func=ACT.Square,
-                    bias=neg_mean[:, slot + half : slot + half + 1],
+                    bias=neg_mean[:, half : half + 1],
                     scale=1.0,
                     accum_out=sum_sq[:, half : half + 1],
                 )
@@ -210,7 +209,7 @@ def tile_functatransformer_pa_t_kernel(
             nc.vector.reciprocal(out=rstd[:], in_=std[:])
             neg_mean_rstd = stats.tile([P, HALVES], F32)
             nc.vector.tensor_tensor(
-                out=neg_mean_rstd[:], in0=neg_mean[:, slot : slot + HALVES], in1=rstd[:], op=ALU.mult
+                out=neg_mean_rstd[:], in0=neg_mean[:], in1=rstd[:], op=ALU.mult
             )
             rstd_of[u] = rstd
             neg_mean_rstd_of[u] = neg_mean_rstd
@@ -311,13 +310,16 @@ def tile_functatransformer_pa_t_kernel(
                         in_=result_of[o][:, h].rearrange("p sj d -> p (sj d)"),
                     )
 
+        def project_some(step, part):
+            for n in range(PASSES_PER_STEP // 2):
+                number = (step % WIN_PER_SIDE) * PASSES_PER_STEP + part * (PASSES_PER_STEP // 2) + n
+                project(step // WIN_PER_SIDE, number // WIN, number % WIN)
+
         for k in range(-1, UNITS + LAG):
             if 0 <= k - 1 < UNITS:
                 channels_to_partitions(k - 1)
             if 0 <= k + 1 < UNITS:
-                if (k + 1) % WIN_PER_SIDE == 0:
-                    means((k + 1) // WIN_PER_SIDE)
-                tokens_to_partitions(k + 1)
+                means(k + 1)
             if 0 <= k < UNITS:
                 variance(k)
             if 0 <= k - 1 < UNITS:
@@ -327,8 +329,10 @@ def tile_functatransformer_pa_t_kernel(
             if 0 <= k < 3:
                 prepare_weight(k)
             if 0 <= k - LAG < UNITS:
-                for n in range(PASSES_PER_STEP):
-                    number = ((k - LAG) % WIN_PER_SIDE) * PASSES_PER_STEP + n
-                    project((k - LAG) // WIN_PER_SIDE, number // WIN, number % WIN)
+                project_some(k - LAG, 0)
+            if 0 <= k + 1 < UNITS:
+                tokens_to_partitions(k + 1)
+            if 0 <= k - LAG < UNITS:
+                project_some(k - LAG, 1)
             if 0 <= k - 1 < UNITS:
                 regroup(k - 1)

@@ -32,6 +32,7 @@ UNITS = BATCH * WIN_PER_SIDE
 PASSES = 3 * WIN
 PASSES_PER_STEP = PASSES // WIN_PER_SIDE
 LAG = WIN_PER_SIDE + 1
+HEAD_BANKS = 7
 
 FLOPS = 2 * BATCH * TOKENS * CHANNELS * 3 * OUT_COLS
 
@@ -62,87 +63,98 @@ def tile_functatransformer_pa_t_kernel(
 
     with ExitStack() as ctx:
         const = ctx.enter_context(tc.tile_pool(name="const", bufs=1))
-        images = ctx.enter_context(tc.tile_pool(name="images", bufs=BATCH))
+        images = ctx.enter_context(tc.tile_pool(name="images", bufs=BATCH - 1))
         wstage = ctx.enter_context(tc.tile_pool(name="wstage", bufs=3))
-        stats = ctx.enter_context(tc.tile_pool(name="stats", bufs=4))
+        stats = ctx.enter_context(tc.tile_pool(name="stats", bufs=6))
         norm = ctx.enter_context(tc.tile_pool(name="norm", bufs=4))
         quant = ctx.enter_context(tc.tile_pool(name="quant", bufs=2))
         results = ctx.enter_context(tc.tile_pool(name="results", bufs=4))
-        psum_x = ctx.enter_context(tc.psum_pool(name="psum_x", bufs=2))
         psum_sum = ctx.enter_context(tc.psum_pool(name="psum_sum", bufs=1))
-        psum_y = ctx.enter_context(tc.psum_pool(name="psum_y", bufs=1))
-        psum_acc = ctx.enter_context(tc.psum_pool(name="psum_acc", bufs=3))
         ctx.enter_context(tc.manual_schedule())
 
-        x_tiles = []
-        for b in range(BATCH):
-            x_sb = images.tile([P, PACK, TOKENS], BF16)
-            x_tiles.append(x_sb)
+        bias_rows = const.tile([P, 3, OUT_COLS], BF16)
+        nc.vector.memset(bias_rows[:], 0.0)
 
-        def load_image(b):
-            nc.sync.dma_start(
-                out=x_tiles[b][:], in_=x[b].rearrange("(p t) i j -> p t (i j)", t=PACK)
-            )
-
-        load_image(0)
+        x_view = [x[b].rearrange("(p t) i j -> p t (i j)", t=PACK) for b in range(BATCH)]
+        piece_bounds = ((P, 2 * P), (3 * P, 2 * P), (5 * P, 3 * P), (0, P))
+        pieces = []
+        for n, (first, count) in enumerate(piece_bounds):
+            piece = const.tile([P, PACK, count], BF16, name="piece%d" % n)
+            nc.sync.dma_start(out=piece[:], in_=x_view[0][:, :, first : first + count])
+            pieces.append(piece)
+            if n < 3:
+                nc.scalar.dma_start(
+                    out=bias_rows[0:1, n, :], in_=biases[n].rearrange("(a n) -> a n", a=1)
+                )
+        w_raw = []
         gain_bf = const.tile([P, PACK], BF16)
         shift_bf = const.tile([P, PACK], BF16)
-        nc.scalar.dma_start(out=gain_bf[:], in_=ln1_g.rearrange("(p t) -> p t", t=PACK))
-        nc.scalar.dma_start(out=shift_bf[:], in_=ln1_b.rearrange("(p t) -> p t", t=PACK))
-        w_raw = []
         for o in range(3):
             raw = wstage.tile([P, PACK, OUT_COLS], BF16)
             nc.sync.dma_start(out=raw[:], in_=weights[o].rearrange("(p t) n -> p t n", t=PACK))
             w_raw.append(raw)
+            if o == 0:
+                nc.sync.dma_start(out=gain_bf[:], in_=ln1_g.rearrange("(p t) -> p t", t=PACK))
+                nc.sync.dma_start(out=shift_bf[:], in_=ln1_b.rearrange("(p t) -> p t", t=PACK))
+        x_tiles = [None]
         for b in range(1, BATCH):
-            load_image(b)
+            x_sb = images.tile([P, PACK, TOKENS], BF16)
+            nc.sync.dma_start(out=x_sb[:], in_=x_view[b])
+            x_tiles.append(x_sb)
 
         eps = const.tile([P, 1], F32)
         nc.vector.memset(eps[:], EPS)
         warm = const.tile([P, 1], F32)
         nc.scalar.activation(out=warm[:], in_=eps[:], func=ACT.Sqrt)
-        ones = const.tile([P, SUM_COLS], BF16)
+        ones = const.tile([P, P], BF16)
         nc.vector.memset(ones[:], 1.0)
         ident_bf = const.tile([P, P], BF16)
         make_identity(nc, ident_bf[:])
         token_sort = build_token_sort(nc, const)
-        bias_bf = []
-        for o in range(3):
-            row = const.tile([P, OUT_COLS], BF16, name="bias_bf%d" % o)
-            nc.gpsimd.dma_start(out=row[:], in_=biases[o].partition_broadcast(P))
-            bias_bf.append(row)
         gain = const.tile([P, PACK], F32)
         shift = const.tile([P, PACK], F32)
-        nc.vector.tensor_copy(out=gain[:], in_=gain_bf[:])
-        nc.vector.tensor_copy(out=shift[:], in_=shift_bf[:])
 
-        w_codes = []
-        w_scales = []
-        bias_f32 = []
+        w_grouped_of = {}
+        w_codes = {}
+        w_scales = {}
+        bias_f32 = {}
 
-        def prepare_weight(o):
+        def group_weight(o):
             w_grouped = wstage.tile([P, OUT_COLS, PACK], BF16, align_bytes=64)
-            nc.vector.tensor_copy(
-                out=w_grouped[:].rearrange("p (c i) t -> p c t i", i=4),
-                in_=w_raw[o][:].rearrange("p t (c i) -> p c t i", i=4),
+            nc.gpsimd.tensor_scalar(
+                out=w_grouped[:],
+                in0=w_raw[o][:].rearrange("p t n -> p n t"),
+                scalar1=1.0,
+                scalar2=0.0,
+                op0=ALU.mult,
+                op1=ALU.add,
             )
-            row = const.tile([P, OUT_COLS], F32, name="bias_f32%d" % o)
-            nc.vector.tensor_scalar(
-                out=row[:], in0=bias_bf[o][:], scalar1=out_scales[o], scalar2=None, op0=ALU.mult
-            )
-            bias_f32.append(row)
+            w_grouped_of[o] = w_grouped
+
+        def quantise_weight(o):
             codes = const.tile([P, OUT_COLS], U32, align_bytes=64, name="w_codes%d" % o)
             scales = const.tile([P, OUT_COLS], U8, align_bytes=64, name="w_scales%d" % o)
             nc.vector.quantize_mx(
                 out=codes[:].bitcast(FP8X4),
                 scales=scales[:],
-                in_=w_grouped[:].rearrange("p n t -> p (n t)"),
+                in_=w_grouped_of[o][:].rearrange("p n t -> p (n t)"),
             )
-            w_codes.append(codes)
-            w_scales.append(scales)
+            w_codes[o] = codes
+            w_scales[o] = scales
+
+        def spread_bias(o, bank):
+            nc.tensor.matmul(
+                out=bank[:], lhsT=ones[:], rhs=bias_rows[:, o, :], start=True, stop=True
+            )
+            row = const.tile([P, OUT_COLS], F32, name="bias_f32%d" % o)
+            nc.vector.tensor_scalar(
+                out=row[:], in0=bank[:], scalar1=out_scales[o], scalar2=None, op0=ALU.mult
+            )
+            bias_f32[o] = row
 
         neg_mean_of = {}
         x_t_of = {}
+        std_of = {}
         rstd_of = {}
         neg_mean_rstd_of = {}
         y_of = {}
@@ -153,19 +165,24 @@ def tile_functatransformer_pa_t_kernel(
         x_scales_of = {}
         result_of = {}
 
-        def first_token(u, half):
+        def x_block(u, half, t):
             a = HALVES * (u % WIN_PER_SIDE) + half
-            return ((a + 1) % TILES) * P
+            first = ((a + 1) % TILES) * P
+            if u >= WIN_PER_SIDE:
+                return x_tiles[u // WIN_PER_SIDE][:, t, first : first + P]
+            for n, (start, count) in enumerate(piece_bounds):
+                if start <= first < start + count:
+                    return pieces[n][:, t, first - start : first - start + P]
+            return None
 
         def means(u):
             sums = psum_sum.tile([P, HALVES, SUM_COLS], F32)
             for half in range(HALVES):
-                first = first_token(u, half)
                 for t in range(PACK):
                     nc.tensor.matmul(
                         out=sums[:, half, :],
-                        lhsT=x_tiles[u // WIN_PER_SIDE][:, t, first : first + P],
-                        rhs=ones[:],
+                        lhsT=x_block(u, half, t),
+                        rhs=ones[:, 0:SUM_COLS],
                         start=(t == 0),
                         stop=(t == PACK - 1),
                     )
@@ -176,19 +193,15 @@ def tile_functatransformer_pa_t_kernel(
             )
             neg_mean_of[u] = neg_mean
 
-        def tokens_to_partitions(u):
-            x_t = psum_x.tile([P, HALVES, PACK, P], BF16)
+        def tokens_to_partitions(u, x_t):
             for half in range(HALVES):
-                first = first_token(u, half)
                 for t in range(PACK):
                     nc.tensor.transpose(
-                        out=x_t[:, half, t, :],
-                        in_=x_tiles[u // WIN_PER_SIDE][:, t, first : first + P],
-                        identity=ident_bf[:],
+                        out=x_t[:, half, t, :], in_=x_block(u, half, t), identity=ident_bf[:]
                     )
             x_t_of[u] = x_t
 
-        def variance(u):
+        def squares_and_std(u):
             neg_mean = neg_mean_of[u]
             sum_sq = stats.tile([P, HALVES], F32)
             for half in range(HALVES):
@@ -205,11 +218,14 @@ def tile_functatransformer_pa_t_kernel(
             nc.scalar.activation(
                 out=std[:], in_=sum_sq[:], func=ACT.Sqrt, bias=eps[:, 0:1], scale=1.0 / CHANNELS
             )
+            std_of[u] = std
+
+        def reciprocal_std(u):
             rstd = stats.tile([P, HALVES], F32)
-            nc.vector.reciprocal(out=rstd[:], in_=std[:])
+            nc.vector.reciprocal(out=rstd[:], in_=std_of[u][:])
             neg_mean_rstd = stats.tile([P, HALVES], F32)
             nc.vector.tensor_tensor(
-                out=neg_mean_rstd[:], in0=neg_mean[:], in1=rstd[:], op=ALU.mult
+                out=neg_mean_rstd[:], in0=neg_mean_of[u][:], in1=rstd[:], op=ALU.mult
             )
             rstd_of[u] = rstd
             neg_mean_rstd_of[u] = neg_mean_rstd
@@ -218,18 +234,26 @@ def tile_functatransformer_pa_t_kernel(
             y_of[u] = []
             for half in range(HALVES):
                 y = norm.tile([P, PACK, P], F32)
-                nc.scalar.activation(
-                    out=y[:].rearrange("p t c -> p (t c)"),
-                    in_=x_t_of[u][:, half].rearrange("p t c -> p (t c)"),
-                    func=ACT.Identity,
-                    bias=neg_mean_rstd_of[u][:, half : half + 1],
-                    scale=rstd_of[u][:, half : half + 1],
-                )
+                if u < WIN_PER_SIDE:
+                    nc.vector.tensor_scalar(
+                        out=y[:].rearrange("p t c -> p (t c)"),
+                        in0=x_t_of[u][:, half].rearrange("p t c -> p (t c)"),
+                        scalar1=rstd_of[u][:, half : half + 1],
+                        scalar2=neg_mean_rstd_of[u][:, half : half + 1],
+                        op0=ALU.mult,
+                        op1=ALU.add,
+                    )
+                else:
+                    nc.scalar.activation(
+                        out=y[:].rearrange("p t c -> p (t c)"),
+                        in_=x_t_of[u][:, half].rearrange("p t c -> p (t c)"),
+                        func=ACT.Identity,
+                        bias=neg_mean_rstd_of[u][:, half : half + 1],
+                        scale=rstd_of[u][:, half : half + 1],
+                    )
                 y_of[u].append(y)
 
-        def channels_to_partitions(u):
-            y_t_low = psum_y.tile([P, 2, HALVES, P], F32)
-            y_t_high = psum_y.tile([P, 2, HALVES, P], F32)
+        def channels_to_partitions(u, y_t_low, y_t_high):
             y_t_of[u] = (y_t_low, y_t_high)
             for half in range(HALVES):
                 for t in range(PACK):
@@ -262,24 +286,69 @@ def tile_functatransformer_pa_t_kernel(
                 grouped = quant.tile([P, WIN, P, PACK], BF16, align_bytes=64)
                 grouped_of[b] = grouped
             per_row = WIN_PER_SIDE * WIN
-            nc.gpsimd.tensor_scalar(
-                out=grouped_of[b][:, :, per_row * wi : per_row * (wi + 1), :],
-                in0=planes_of[u][:].rearrange("p t (sj c) -> p sj c t", sj=WIN),
-                scalar1=1.0,
-                scalar2=0.0,
-                op0=ALU.mult,
-                op1=ALU.add,
-            )
-            if wi == WIN_PER_SIDE - 1:
-                x_codes = quant.tile([P, WIN * P], U32, align_bytes=64)
-                x_scales = quant.tile([P, WIN * P], U8, align_bytes=64)
-                nc.vector.quantize_mx(
-                    out=x_codes[:].bitcast(FP8X4),
-                    scales=x_scales[:],
-                    in_=grouped_of[b][:].rearrange("p sj m t -> p (sj m t)"),
+            mine = grouped_of[b][:, :, per_row * wi : per_row * (wi + 1), :]
+            if b == 0:
+                nc.vector.tensor_copy(
+                    out=mine.rearrange("p sj (c i) t -> p sj c t i", i=4),
+                    in_=planes_of[u][:].rearrange("p t (sj c i) -> p sj c t i", sj=WIN, i=4),
                 )
-                x_codes_of[b] = x_codes
-                x_scales_of[b] = x_scales
+            else:
+                nc.gpsimd.tensor_scalar(
+                    out=mine,
+                    in0=planes_of[u][:].rearrange("p t (sj c) -> p sj c t", sj=WIN),
+                    scalar1=1.0,
+                    scalar2=0.0,
+                    op0=ALU.mult,
+                    op1=ALU.add,
+                )
+
+        def quantise_image(b):
+            x_codes = quant.tile([P, WIN * P], U32, align_bytes=64)
+            x_scales = quant.tile([P, WIN * P], U8, align_bytes=64)
+            nc.vector.quantize_mx(
+                out=x_codes[:].bitcast(FP8X4),
+                scales=x_scales[:],
+                in_=grouped_of[b][:].rearrange("p sj m t -> p (sj m t)"),
+            )
+            x_codes_of[b] = x_codes
+            x_scales_of[b] = x_scales
+
+        with tc.psum_pool(name="psum_head", bufs=HEAD_BANKS) as psum_head:
+            for u in range(WIN_PER_SIDE):
+                means(u)
+                x_head = psum_head.tile([P, HALVES, PACK, P], BF16, name="head_bank")
+                tokens_to_partitions(u, x_head)
+                if u < 3:
+                    bias_bank = psum_head.tile([P, OUT_COLS], F32, name="head_bank")
+                    spread_bias(u, bias_bank)
+            group_weight(0)
+            group_weight(1)
+            for u in range(WIN_PER_SIDE + 1):
+                if u == 2:
+                    nc.vector.tensor_copy(out=gain[:], in_=gain_bf[:])
+                    nc.vector.tensor_copy(out=shift[:], in_=shift_bf[:])
+                if u < WIN_PER_SIDE:
+                    squares_and_std(u)
+                    reciprocal_std(u)
+                    normalise(u)
+                if u == WIN_PER_SIDE:
+                    gain_and_shift(0)
+                    regroup(0)
+                    quantise_weight(0)
+                if u >= 1:
+                    low_head = psum_head.tile([P, 2, HALVES, P], F32, name="head_bank")
+                    high_head = psum_head.tile([P, 2, HALVES, P], F32, name="head_bank")
+                    channels_to_partitions(u - 1, low_head, high_head)
+            means(WIN_PER_SIDE)
+            for u in range(1, WIN_PER_SIDE):
+                gain_and_shift(u)
+                regroup(u)
+                if u == 1:
+                    quantise_weight(1)
+
+        psum_x = ctx.enter_context(tc.psum_pool(name="psum_x", bufs=2))
+        psum_y = ctx.enter_context(tc.psum_pool(name="psum_y", bufs=1))
+        psum_acc = ctx.enter_context(tc.psum_pool(name="psum_acc", bufs=3))
 
         def project(b, o, sj):
             if sj == 0:
@@ -310,29 +379,47 @@ def tile_functatransformer_pa_t_kernel(
                         in_=result_of[o][:, h].rearrange("p sj d -> p (sj d)"),
                     )
 
-        def project_some(step, part):
-            for n in range(PASSES_PER_STEP // 2):
-                number = (step % WIN_PER_SIDE) * PASSES_PER_STEP + part * (PASSES_PER_STEP // 2) + n
-                project(step // WIN_PER_SIDE, number // WIN, number % WIN)
+        passes_of_step = {}
+        for number in range(PASSES):
+            passes_of_step.setdefault(WIN_PER_SIDE + number // 5, []).append((0, number))
+        for b in range(1, BATCH):
+            for number in range(PASSES):
+                step = WIN_PER_SIDE * b + LAG + number // PASSES_PER_STEP
+                passes_of_step.setdefault(step, []).append((b, number))
 
-        for k in range(-1, UNITS + LAG):
-            if 0 <= k - 1 < UNITS:
-                channels_to_partitions(k - 1)
-            if 0 <= k + 1 < UNITS:
+        def project_some(k, part):
+            mine = passes_of_step.get(k, [])
+            cut = (len(mine) + 1) // 2
+            for b, number in mine[:cut] if part == 0 else mine[cut:]:
+                project(b, number // WIN, number % WIN)
+
+        x_t = psum_x.tile([P, HALVES, PACK, P], BF16)
+        tokens_to_partitions(WIN_PER_SIDE, x_t)
+        quantise_image(0)
+        group_weight(2)
+        for k in range(WIN_PER_SIDE, UNITS + LAG):
+            behind = WIN_PER_SIDE <= k - 1 < UNITS
+            if behind:
+                y_t_low = psum_y.tile([P, 2, HALVES, P], F32)
+                y_t_high = psum_y.tile([P, 2, HALVES, P], F32)
+                channels_to_partitions(k - 1, y_t_low, y_t_high)
+            if k + 1 < UNITS:
                 means(k + 1)
-            if 0 <= k < UNITS:
-                variance(k)
-            if 0 <= k - 1 < UNITS:
+            if k < UNITS:
+                squares_and_std(k)
+            if behind:
                 gain_and_shift(k - 1)
-            if 0 <= k < UNITS:
+            if k < UNITS:
+                reciprocal_std(k)
                 normalise(k)
-            if 0 <= k < 3:
-                prepare_weight(k)
-            if 0 <= k - LAG < UNITS:
-                project_some(k - LAG, 0)
-            if 0 <= k + 1 < UNITS:
-                tokens_to_partitions(k + 1)
-            if 0 <= k - LAG < UNITS:
-                project_some(k - LAG, 1)
-            if 0 <= k - 1 < UNITS:
+            project_some(k, 0)
+            if k + 1 < UNITS:
+                x_t = psum_x.tile([P, HALVES, PACK, P], BF16)
+                tokens_to_partitions(k + 1, x_t)
+            project_some(k, 1)
+            if k == WIN_PER_SIDE:
+                quantise_weight(2)
+            if behind:
                 regroup(k - 1)
+                if k % WIN_PER_SIDE == 0:
+                    quantise_image(k // WIN_PER_SIDE - 1)

@@ -33,6 +33,7 @@ PASSES = 3 * WIN
 PASSES_PER_STEP = PASSES // WIN_PER_SIDE
 LAG = WIN_PER_SIDE + 1
 HEAD_BANKS = 7
+GPSIMD_COLS = 128
 
 FLOPS = 2 * BATCH * TOKENS * CHANNELS * 3 * OUT_COLS
 
@@ -119,16 +120,19 @@ def tile_functatransformer_pa_t_kernel(
         w_scales = {}
         bias_f32 = {}
 
+        def gpsimd_move(out, in_):
+            nc.gpsimd.tensor_scalar(
+                out=out, in0=in_, scalar1=1.0, scalar2=0.0, op0=ALU.mult, op1=ALU.add
+            )
+
         def group_weight(o):
             w_grouped = wstage.tile([P, OUT_COLS, PACK], BF16, align_bytes=64)
-            nc.gpsimd.tensor_scalar(
-                out=w_grouped[:],
-                in0=w_raw[o][:].rearrange("p t n -> p n t"),
-                scalar1=1.0,
-                scalar2=0.0,
-                op0=ALU.mult,
-                op1=ALU.add,
-            )
+            side_by_side = w_raw[o][:].rearrange("p t n -> p n t")
+            for first in range(0, OUT_COLS, GPSIMD_COLS):
+                gpsimd_move(
+                    w_grouped[:, first : first + GPSIMD_COLS, :],
+                    side_by_side[:, first : first + GPSIMD_COLS, :],
+                )
             w_grouped_of[o] = w_grouped
 
         def quantise_weight(o):
@@ -223,12 +227,13 @@ def tile_functatransformer_pa_t_kernel(
         def reciprocal_std(u):
             rstd = stats.tile([P, HALVES], F32)
             nc.vector.reciprocal(out=rstd[:], in_=std_of[u][:])
-            neg_mean_rstd = stats.tile([P, HALVES], F32)
-            nc.vector.tensor_tensor(
-                out=neg_mean_rstd[:], in0=neg_mean_of[u][:], in1=rstd[:], op=ALU.mult
-            )
             rstd_of[u] = rstd
-            neg_mean_rstd_of[u] = neg_mean_rstd
+            if u >= WIN_PER_SIDE:
+                neg_mean_rstd = stats.tile([P, HALVES], F32)
+                nc.vector.tensor_tensor(
+                    out=neg_mean_rstd[:], in0=neg_mean_of[u][:], in1=rstd[:], op=ALU.mult
+                )
+                neg_mean_rstd_of[u] = neg_mean_rstd
 
         def normalise(u):
             y_of[u] = []
@@ -238,10 +243,10 @@ def tile_functatransformer_pa_t_kernel(
                     nc.vector.tensor_scalar(
                         out=y[:].rearrange("p t c -> p (t c)"),
                         in0=x_t_of[u][:, half].rearrange("p t c -> p (t c)"),
-                        scalar1=rstd_of[u][:, half : half + 1],
-                        scalar2=neg_mean_rstd_of[u][:, half : half + 1],
-                        op0=ALU.mult,
-                        op1=ALU.add,
+                        scalar1=neg_mean_of[u][:, half : half + 1],
+                        scalar2=rstd_of[u][:, half : half + 1],
+                        op0=ALU.add,
+                        op1=ALU.mult,
                     )
                 else:
                     nc.scalar.activation(
@@ -266,17 +271,22 @@ def tile_functatransformer_pa_t_kernel(
         def gain_and_shift(u):
             planes = norm.tile([P, PACK, HALVES * P], BF16)
             for t in range(PACK):
-                nc.scalar.activation(
-                    out=planes[:, t, :].rearrange(
-                        "p (g half r) -> p g half r", half=HALVES, r=TILE_ROWS
-                    ),
-                    in_=y_t_of[u][t // 2][:, t % 2].rearrange(
-                        "p half (g r) -> p g half r", r=TILE_ROWS
-                    ),
-                    func=ACT.Identity,
-                    bias=shift[:, t : t + 1],
-                    scale=gain[:, t : t + 1],
+                sorted_out = planes[:, t, :].rearrange(
+                    "p (g half r) -> p g half r", half=HALVES, r=TILE_ROWS
                 )
+                sorted_in = y_t_of[u][t // 2][:, t % 2].rearrange(
+                    "p half (g r) -> p g half r", r=TILE_ROWS
+                )
+                if u == WIN_PER_SIDE - 1:
+                    nc.vector.tensor_scalar(
+                        out=sorted_out, in0=sorted_in, scalar1=gain[:, t : t + 1],
+                        scalar2=shift[:, t : t + 1], op0=ALU.mult, op1=ALU.add,
+                    )
+                else:
+                    nc.scalar.activation(
+                        out=sorted_out, in_=sorted_in, func=ACT.Identity,
+                        bias=shift[:, t : t + 1], scale=gain[:, t : t + 1],
+                    )
             planes_of[u] = planes
 
         def regroup(u):
@@ -287,20 +297,16 @@ def tile_functatransformer_pa_t_kernel(
                 grouped_of[b] = grouped
             per_row = WIN_PER_SIDE * WIN
             mine = grouped_of[b][:, :, per_row * wi : per_row * (wi + 1), :]
-            if b == 0:
-                nc.vector.tensor_copy(
-                    out=mine.rearrange("p sj (c i) t -> p sj c t i", i=4),
-                    in_=planes_of[u][:].rearrange("p t (sj c i) -> p sj c t i", sj=WIN, i=4),
-                )
+            side_by_side = planes_of[u][:].rearrange("p t (sj c) -> p sj c t", sj=WIN)
+            if u == WIN_PER_SIDE - 2:
+                nc.scalar.copy(out=mine, in_=side_by_side)
+            elif u == WIN_PER_SIDE - 1:
+                nc.vector.tensor_copy(out=mine, in_=side_by_side)
             else:
-                nc.gpsimd.tensor_scalar(
-                    out=mine,
-                    in0=planes_of[u][:].rearrange("p t (sj c) -> p sj c t", sj=WIN),
-                    scalar1=1.0,
-                    scalar2=0.0,
-                    op0=ALU.mult,
-                    op1=ALU.add,
-                )
+                for sj in range(0, WIN, WIN // 2):
+                    gpsimd_move(
+                        mine[:, sj : sj + WIN // 2], side_by_side[:, sj : sj + WIN // 2]
+                    )
 
         def quantise_image(b):
             x_codes = quant.tile([P, WIN * P], U32, align_bytes=64)
@@ -318,13 +324,12 @@ def tile_functatransformer_pa_t_kernel(
                 means(u)
                 x_head = psum_head.tile([P, HALVES, PACK, P], BF16, name="head_bank")
                 tokens_to_partitions(u, x_head)
-                if u < 3:
-                    bias_bank = psum_head.tile([P, OUT_COLS], F32, name="head_bank")
-                    spread_bias(u, bias_bank)
+            bias_bank = psum_head.tile([P, OUT_COLS], F32, name="head_bank")
+            spread_bias(0, bias_bank)
             group_weight(0)
-            group_weight(1)
             for u in range(WIN_PER_SIDE + 1):
                 if u == 2:
+                    quantise_weight(0)
                     nc.vector.tensor_copy(out=gain[:], in_=gain_bf[:])
                     nc.vector.tensor_copy(out=shift[:], in_=shift_bf[:])
                 if u < WIN_PER_SIDE:
@@ -334,17 +339,17 @@ def tile_functatransformer_pa_t_kernel(
                 if u == WIN_PER_SIDE:
                     gain_and_shift(0)
                     regroup(0)
-                    quantise_weight(0)
                 if u >= 1:
                     low_head = psum_head.tile([P, 2, HALVES, P], F32, name="head_bank")
                     high_head = psum_head.tile([P, 2, HALVES, P], F32, name="head_bank")
                     channels_to_partitions(u - 1, low_head, high_head)
             means(WIN_PER_SIDE)
-            for u in range(1, WIN_PER_SIDE):
-                gain_and_shift(u)
-                regroup(u)
-                if u == 1:
-                    quantise_weight(1)
+            gain_and_shift(1)
+            regroup(1)
+            gain_and_shift(3)
+            gain_and_shift(2)
+            regroup(2)
+            regroup(3)
 
         psum_x = ctx.enter_context(tc.psum_pool(name="psum_x", bufs=2))
         psum_y = ctx.enter_context(tc.psum_pool(name="psum_y", bufs=1))
@@ -396,6 +401,7 @@ def tile_functatransformer_pa_t_kernel(
         x_t = psum_x.tile([P, HALVES, PACK, P], BF16)
         tokens_to_partitions(WIN_PER_SIDE, x_t)
         quantise_image(0)
+        group_weight(1)
         group_weight(2)
         for k in range(WIN_PER_SIDE, UNITS + LAG):
             behind = WIN_PER_SIDE <= k - 1 < UNITS
@@ -413,12 +419,15 @@ def tile_functatransformer_pa_t_kernel(
                 reciprocal_std(k)
                 normalise(k)
             project_some(k, 0)
+            if k - WIN_PER_SIDE in (0, 1):
+                acc = psum_acc.tile([P, OUT_COLS], F32)
+                spread_bias(k - WIN_PER_SIDE + 1, acc)
             if k + 1 < UNITS:
                 x_t = psum_x.tile([P, HALVES, PACK, P], BF16)
                 tokens_to_partitions(k + 1, x_t)
             project_some(k, 1)
-            if k == WIN_PER_SIDE:
-                quantise_weight(2)
+            if k - WIN_PER_SIDE in (0, 1):
+                quantise_weight(k - WIN_PER_SIDE + 1)
             if behind:
                 regroup(k - 1)
                 if k % WIN_PER_SIDE == 0:

@@ -27,12 +27,15 @@ EPS = 1e-5
 TILE_ROWS = P // SIDE
 TILES = TOKENS // P
 HALVES = WIN // TILE_ROWS
-SUM_COLS = 32
+SUM_COLS = 8
+HEAD_SUM_COLS = 128
 UNITS = BATCH * WIN_PER_SIDE
 PASSES = 3 * WIN
 PASSES_PER_STEP = PASSES // WIN_PER_SIDE
 LAG = WIN_PER_SIDE + 1
-HEAD_BANKS = 7
+HEAD_BANKS = 6
+WARM_UP = 4
+KEEP_WARM = 2
 GPSIMD_COLS = 128
 
 FLOPS = 2 * BATCH * TOKENS * CHANNELS * 3 * OUT_COLS
@@ -107,7 +110,7 @@ def tile_functatransformer_pa_t_kernel(
         nc.vector.memset(eps[:], EPS)
         warm = const.tile([P, 1], F32)
         nc.scalar.activation(out=warm[:], in_=eps[:], func=ACT.Sqrt)
-        ones = const.tile([P, P], BF16)
+        ones = const.tile([P, OUT_COLS], BF16)
         nc.vector.memset(ones[:], 1.0)
         ident_bf = const.tile([P, P], BF16)
         make_identity(nc, ident_bf[:])
@@ -148,7 +151,7 @@ def tile_functatransformer_pa_t_kernel(
 
         def spread_bias(o, bank):
             nc.tensor.matmul(
-                out=bank[:], lhsT=ones[:], rhs=bias_rows[:, o, :], start=True, stop=True
+                out=bank[:], lhsT=ones[:, 0:P], rhs=bias_rows[:, o, :], start=True, stop=True
             )
             row = const.tile([P, OUT_COLS], F32, name="bias_f32%d" % o)
             nc.vector.tensor_scalar(
@@ -180,13 +183,14 @@ def tile_functatransformer_pa_t_kernel(
             return None
 
         def means(u):
-            sums = psum_sum.tile([P, HALVES, SUM_COLS], F32)
+            cols = HEAD_SUM_COLS if u <= WIN_PER_SIDE else SUM_COLS
+            sums = psum_sum.tile([P, HALVES, cols], F32)
             for half in range(HALVES):
                 for t in range(PACK):
                     nc.tensor.matmul(
                         out=sums[:, half, :],
                         lhsT=x_block(u, half, t),
-                        rhs=ones[:, 0:SUM_COLS],
+                        rhs=ones[:, 0:cols],
                         start=(t == 0),
                         stop=(t == PACK - 1),
                     )
@@ -200,9 +204,16 @@ def tile_functatransformer_pa_t_kernel(
         def tokens_to_partitions(u, x_t):
             for half in range(HALVES):
                 for t in range(PACK):
-                    nc.tensor.transpose(
-                        out=x_t[:, half, t, :], in_=x_block(u, half, t), identity=ident_bf[:]
-                    )
+                    if u <= WIN_PER_SIDE:
+                        nc.tensor.matmul(
+                            out=x_t[:, half, t, :], lhsT=x_block(u, half, t), rhs=ident_bf[:],
+                            start=True, stop=True,
+                        )
+                    else:
+                        nc.tensor.transpose(
+                            out=x_t[:, half, t, :], in_=x_block(u, half, t),
+                            identity=ident_bf[:],
+                        )
             x_t_of[u] = x_t
 
         def squares_and_std(u):
@@ -319,7 +330,18 @@ def tile_functatransformer_pa_t_kernel(
             x_codes_of[b] = x_codes
             x_scales_of[b] = x_scales
 
-        with tc.psum_pool(name="psum_head", bufs=HEAD_BANKS) as psum_head:
+        with ExitStack() as head:
+            psum_idle = head.enter_context(tc.psum_pool(name="psum_idle", bufs=1))
+            psum_head = head.enter_context(tc.psum_pool(name="psum_head", bufs=HEAD_BANKS))
+            idle_bank = psum_idle.tile([P, OUT_COLS], F32)
+
+            def idle_matmuls(count):
+                for n in range(count):
+                    nc.tensor.matmul(
+                        out=idle_bank[:], lhsT=ones[:, 0:P], rhs=ones[:], start=True, stop=True
+                    )
+
+            idle_matmuls(WARM_UP)
             for u in range(WIN_PER_SIDE):
                 means(u)
                 x_head = psum_head.tile([P, HALVES, PACK, P], BF16, name="head_bank")
@@ -343,6 +365,7 @@ def tile_functatransformer_pa_t_kernel(
                     low_head = psum_head.tile([P, 2, HALVES, P], F32, name="head_bank")
                     high_head = psum_head.tile([P, 2, HALVES, P], F32, name="head_bank")
                     channels_to_partitions(u - 1, low_head, high_head)
+                    idle_matmuls(KEEP_WARM)
             means(WIN_PER_SIDE)
             gain_and_shift(1)
             regroup(1)

@@ -28,14 +28,15 @@ TILE_ROWS = P // SIDE
 TILES = TOKENS // P
 HALVES = WIN // TILE_ROWS
 SUM_COLS = 8
-HEAD_SUM_COLS = 128
 UNITS = BATCH * WIN_PER_SIDE
 PASSES = 3 * WIN
-PASSES_PER_STEP = PASSES // WIN_PER_SIDE
-LAG = WIN_PER_SIDE + 1
-HEAD_BANKS = 6
-WARM_UP = 4
-KEEP_WARM = 2
+WARM_UP = 3
+HEAD_X_BANKS = (0, 1, 2, 0)
+X_BANKS = (0, 1, 2)
+HEAD_Y_BANKS = ((3, 4), (5, 6), (3, 4), (1, 2))
+Y_BANKS = (3, 4)
+ACC_BANKS = (5, 6, 7)
+SUM_BANK = 7
 GPSIMD_COLS = 128
 
 FLOPS = 2 * BATCH * TOKENS * CHANNELS * 3 * OUT_COLS
@@ -73,11 +74,13 @@ def tile_functatransformer_pa_t_kernel(
         norm = ctx.enter_context(tc.tile_pool(name="norm", bufs=4))
         quant = ctx.enter_context(tc.tile_pool(name="quant", bufs=2))
         results = ctx.enter_context(tc.tile_pool(name="results", bufs=4))
-        psum_sum = ctx.enter_context(tc.psum_pool(name="psum_sum", bufs=1))
+        psum = ctx.enter_context(tc.psum_pool(name="psum", bufs=1))
         ctx.enter_context(tc.manual_schedule())
 
-        bias_rows = const.tile([P, 3, OUT_COLS], BF16)
-        nc.vector.memset(bias_rows[:], 0.0)
+        ones = const.tile([P, OUT_COLS], BF16)
+        nc.vector.memset(ones[:], 1.0)
+        eps = const.tile([P, 1], F32)
+        nc.vector.memset(eps[:], EPS)
 
         x_view = [x[b].rearrange("(p t) i j -> p t (i j)", t=PACK) for b in range(BATCH)]
         piece_bounds = ((P, 2 * P), (3 * P, 2 * P), (5 * P, 3 * P), (0, P))
@@ -86,32 +89,40 @@ def tile_functatransformer_pa_t_kernel(
             piece = const.tile([P, PACK, count], BF16, name="piece%d" % n)
             nc.sync.dma_start(out=piece[:], in_=x_view[0][:, :, first : first + count])
             pieces.append(piece)
-            if n < 3:
-                nc.scalar.dma_start(
-                    out=bias_rows[0:1, n, :], in_=biases[n].rearrange("(a n) -> a n", a=1)
-                )
-        w_raw = []
         gain_bf = const.tile([P, PACK], BF16)
         shift_bf = const.tile([P, PACK], BF16)
-        for o in range(3):
-            raw = wstage.tile([P, PACK, OUT_COLS], BF16)
+        nc.sync.dma_start(out=gain_bf[:], in_=ln1_g.rearrange("(p t) -> p t", t=PACK))
+        nc.sync.dma_start(out=shift_bf[:], in_=ln1_b.rearrange("(p t) -> p t", t=PACK))
+        w_raw = []
+        x_tiles = [None]
+        bias_of = []
+
+        def load_weight(o):
+            raw = wstage.tile([P, PACK, OUT_COLS], BF16, name="w_raw")
             nc.sync.dma_start(out=raw[:], in_=weights[o].rearrange("(p t) n -> p t n", t=PACK))
             w_raw.append(raw)
-            if o == 0:
-                nc.sync.dma_start(out=gain_bf[:], in_=ln1_g.rearrange("(p t) -> p t", t=PACK))
-                nc.sync.dma_start(out=shift_bf[:], in_=ln1_b.rearrange("(p t) -> p t", t=PACK))
-        x_tiles = [None]
-        for b in range(1, BATCH):
-            x_sb = images.tile([P, PACK, TOKENS], BF16)
+
+        def load_image(b):
+            x_sb = images.tile([P, PACK, TOKENS], BF16, name="x_sb")
             nc.sync.dma_start(out=x_sb[:], in_=x_view[b])
             x_tiles.append(x_sb)
 
-        eps = const.tile([P, 1], F32)
-        nc.vector.memset(eps[:], EPS)
+        def load_bias(o):
+            bias_bf = const.tile([P, OUT_COLS], BF16, name="bias_bf%d" % o)
+            nc.sync.dma_start(out=bias_bf[:], in_=biases[o].partition_broadcast(P))
+            bias_of.append(bias_bf)
+
+        load_weight(0)
+        load_image(1)
+        for o in range(3):
+            load_bias(o)
+        load_weight(1)
+        load_weight(2)
+        load_image(2)
+        load_image(3)
+
         warm = const.tile([P, 1], F32)
         nc.scalar.activation(out=warm[:], in_=eps[:], func=ACT.Sqrt)
-        ones = const.tile([P, OUT_COLS], BF16)
-        nc.vector.memset(ones[:], 1.0)
         ident_bf = const.tile([P, P], BF16)
         make_identity(nc, ident_bf[:])
         token_sort = build_token_sort(nc, const)
@@ -121,12 +132,16 @@ def tile_functatransformer_pa_t_kernel(
         w_grouped_of = {}
         w_codes = {}
         w_scales = {}
-        bias_f32 = {}
 
-        def gpsimd_move(out, in_):
+        def gpsimd_move(out, in_, factor=1.0):
             nc.gpsimd.tensor_scalar(
-                out=out, in0=in_, scalar1=1.0, scalar2=0.0, op0=ALU.mult, op1=ALU.add
+                out=out, in0=in_, scalar1=factor, scalar2=0.0, op0=ALU.mult, op1=ALU.add
             )
+
+        def scale_bias(o):
+            scaled = const.tile([P, OUT_COLS], F32, name="bias_scaled")
+            gpsimd_move(scaled[:], bias_of[o][:], factor=out_scales[o])
+            bias_of[o] = scaled
 
         def group_weight(o):
             w_grouped = wstage.tile([P, OUT_COLS, PACK], BF16, align_bytes=64)
@@ -149,15 +164,14 @@ def tile_functatransformer_pa_t_kernel(
             w_codes[o] = codes
             w_scales[o] = scales
 
-        def spread_bias(o, bank):
-            nc.tensor.matmul(
-                out=bank[:], lhsT=ones[:, 0:P], rhs=bias_rows[:, o, :], start=True, stop=True
-            )
-            row = const.tile([P, OUT_COLS], F32, name="bias_f32%d" % o)
-            nc.vector.tensor_scalar(
-                out=row[:], in0=bank[:], scalar1=out_scales[o], scalar2=None, op0=ALU.mult
-            )
-            bias_f32[o] = row
+        def bank(number, shape, dtype):
+            return psum.tile(shape, dtype, name="bank%d" % number)
+
+        acc_count = []
+
+        def next_acc(shape):
+            acc_count.append(None)
+            return bank(ACC_BANKS[(len(acc_count) - 1) % len(ACC_BANKS)], shape, F32)
 
         neg_mean_of = {}
         x_t_of = {}
@@ -182,26 +196,34 @@ def tile_functatransformer_pa_t_kernel(
                     return pieces[n][:, t, first - start : first - start + P]
             return None
 
-        def means(u):
-            cols = HEAD_SUM_COLS if u <= WIN_PER_SIDE else SUM_COLS
-            sums = psum_sum.tile([P, HALVES, cols], F32)
-            for half in range(HALVES):
-                for t in range(PACK):
-                    nc.tensor.matmul(
-                        out=sums[:, half, :],
-                        lhsT=x_block(u, half, t),
-                        rhs=ones[:, 0:cols],
-                        start=(t == 0),
-                        stop=(t == PACK - 1),
-                    )
-            neg_mean = stats.tile([P, HALVES], F32)
-            nc.vector.tensor_scalar(
-                out=neg_mean[:], in0=sums[:, :, 0], scalar1=-1.0 / CHANNELS, scalar2=None,
-                op0=ALU.mult,
-            )
-            neg_mean_of[u] = neg_mean
+        def sums(units, tile, place):
+            for n, u in enumerate(units):
+                for half in range(HALVES):
+                    for t in range(PACK):
+                        nc.tensor.matmul(
+                            out=tile[:, place + n, half, :],
+                            lhsT=x_block(u, half, t),
+                            rhs=ones[:, 0:SUM_COLS],
+                            start=(t == 0),
+                            stop=(t == PACK - 1),
+                        )
 
-        def tokens_to_partitions(u, x_t):
+        def negate_means(units, tile, place):
+            neg_mean = stats.tile([P, WIN_PER_SIDE, HALVES], F32)
+            count = len(units)
+            nc.vector.tensor_scalar(
+                out=neg_mean[:, 0:count], in0=tile[:, place : place + count, :, 0],
+                scalar1=-1.0 / CHANNELS, scalar2=None, op0=ALU.mult,
+            )
+            for n, u in enumerate(units):
+                neg_mean_of[u] = neg_mean[:, n]
+
+        def tokens_to_partitions(u):
+            if u < WIN_PER_SIDE:
+                number = HEAD_X_BANKS[u]
+            else:
+                number = X_BANKS[(u - WIN_PER_SIDE) % len(X_BANKS)]
+            x_t = bank(number, [P, HALVES, PACK, P], BF16)
             for half in range(HALVES):
                 for t in range(PACK):
                     if u <= WIN_PER_SIDE:
@@ -217,7 +239,6 @@ def tile_functatransformer_pa_t_kernel(
             x_t_of[u] = x_t
 
         def squares_and_std(u):
-            neg_mean = neg_mean_of[u]
             sum_sq = stats.tile([P, HALVES], F32)
             for half in range(HALVES):
                 squares = norm.tile([P, CHANNELS], BF16)
@@ -225,7 +246,7 @@ def tile_functatransformer_pa_t_kernel(
                     out=squares[:],
                     in_=x_t_of[u][:, half].rearrange("p t c -> p (t c)"),
                     func=ACT.Square,
-                    bias=neg_mean[:, half : half + 1],
+                    bias=neg_mean_of[u][:, half : half + 1],
                     scale=1.0,
                     accum_out=sum_sq[:, half : half + 1],
                 )
@@ -242,7 +263,7 @@ def tile_functatransformer_pa_t_kernel(
             if u >= WIN_PER_SIDE:
                 neg_mean_rstd = stats.tile([P, HALVES], F32)
                 nc.vector.tensor_tensor(
-                    out=neg_mean_rstd[:], in0=neg_mean_of[u][:], in1=rstd[:], op=ALU.mult
+                    out=neg_mean_rstd[:], in0=neg_mean_of[u], in1=rstd[:], op=ALU.mult
                 )
                 neg_mean_rstd_of[u] = neg_mean_rstd
 
@@ -269,26 +290,29 @@ def tile_functatransformer_pa_t_kernel(
                     )
                 y_of[u].append(y)
 
-        def channels_to_partitions(u, y_t_low, y_t_high):
-            y_t_of[u] = (y_t_low, y_t_high)
-            for half in range(HALVES):
-                for t in range(PACK):
+        def channels_to_partitions(u):
+            numbers = HEAD_Y_BANKS[u] if u < WIN_PER_SIDE else Y_BANKS
+            y_t_of[u] = [bank(number, [P, 2, HALVES, P], F32) for number in numbers]
+            for t in range(PACK):
+                for half in range(HALVES):
                     nc.tensor.transpose(
                         out=y_t_of[u][t // 2][:, t % 2, half, :],
                         in_=y_of[u][half][:, t, :],
                         identity=token_sort[:],
                     )
 
-        def gain_and_shift(u):
-            planes = norm.tile([P, PACK, HALVES * P], BF16)
-            for t in range(PACK):
-                sorted_out = planes[:, t, :].rearrange(
+        def gain_and_shift(u, slots, on_vector):
+            if u not in planes_of:
+                planes = norm.tile([P, PACK, HALVES * P], BF16)
+                planes_of[u] = planes
+            for t in slots:
+                sorted_out = planes_of[u][:, t, :].rearrange(
                     "p (g half r) -> p g half r", half=HALVES, r=TILE_ROWS
                 )
                 sorted_in = y_t_of[u][t // 2][:, t % 2].rearrange(
                     "p half (g r) -> p g half r", r=TILE_ROWS
                 )
-                if u == WIN_PER_SIDE - 1:
+                if on_vector:
                     nc.vector.tensor_scalar(
                         out=sorted_out, in0=sorted_in, scalar1=gain[:, t : t + 1],
                         scalar2=shift[:, t : t + 1], op0=ALU.mult, op1=ALU.add,
@@ -298,91 +322,44 @@ def tile_functatransformer_pa_t_kernel(
                         out=sorted_out, in_=sorted_in, func=ACT.Identity,
                         bias=shift[:, t : t + 1], scale=gain[:, t : t + 1],
                     )
-            planes_of[u] = planes
 
-        def regroup(u):
+        def regroup(u, part, engine):
             b = u // WIN_PER_SIDE
             wi = u % WIN_PER_SIDE
-            if wi == 0:
+            if b not in grouped_of:
                 grouped = quant.tile([P, WIN, P, PACK], BF16, align_bytes=64)
                 grouped_of[b] = grouped
             per_row = WIN_PER_SIDE * WIN
-            mine = grouped_of[b][:, :, per_row * wi : per_row * (wi + 1), :]
-            side_by_side = planes_of[u][:].rearrange("p t (sj c) -> p sj c t", sj=WIN)
-            if u == WIN_PER_SIDE - 2:
-                nc.scalar.copy(out=mine, in_=side_by_side)
-            elif u == WIN_PER_SIDE - 1:
+            cols = slice(part * WIN // 2, (part + 1) * WIN // 2)
+            mine = grouped_of[b][:, cols, per_row * wi : per_row * (wi + 1), :]
+            side_by_side = planes_of[u][:].rearrange("p t (sj c) -> p sj c t", sj=WIN)[:, cols]
+            if engine == "vector":
                 nc.vector.tensor_copy(out=mine, in_=side_by_side)
+            elif engine == "scalar":
+                nc.scalar.copy(out=mine, in_=side_by_side)
             else:
-                for sj in range(0, WIN, WIN // 2):
-                    gpsimd_move(
-                        mine[:, sj : sj + WIN // 2], side_by_side[:, sj : sj + WIN // 2]
-                    )
+                gpsimd_move(mine, side_by_side)
 
-        def quantise_image(b):
-            x_codes = quant.tile([P, WIN * P], U32, align_bytes=64)
-            x_scales = quant.tile([P, WIN * P], U8, align_bytes=64)
+        def quantise_half(b, part):
+            if part == 0:
+                x_codes = quant.tile([P, WIN * P], U32, align_bytes=64)
+                x_scales = quant.tile([P, WIN * P], U8, align_bytes=64)
+                x_codes_of[b] = x_codes
+                x_scales_of[b] = x_scales
+            cols = slice(part * WIN // 2 * P, (part + 1) * WIN // 2 * P)
             nc.vector.quantize_mx(
-                out=x_codes[:].bitcast(FP8X4),
-                scales=x_scales[:],
-                in_=grouped_of[b][:].rearrange("p sj m t -> p (sj m t)"),
+                out=x_codes_of[b][:, cols].bitcast(FP8X4),
+                scales=x_scales_of[b][:, cols],
+                in_=grouped_of[b][:, part * WIN // 2 : (part + 1) * WIN // 2].rearrange(
+                    "p sj m t -> p (sj m t)"
+                ),
             )
-            x_codes_of[b] = x_codes
-            x_scales_of[b] = x_scales
-
-        with ExitStack() as head:
-            psum_idle = head.enter_context(tc.psum_pool(name="psum_idle", bufs=1))
-            psum_head = head.enter_context(tc.psum_pool(name="psum_head", bufs=HEAD_BANKS))
-            idle_bank = psum_idle.tile([P, OUT_COLS], F32)
-
-            def idle_matmuls(count):
-                for n in range(count):
-                    nc.tensor.matmul(
-                        out=idle_bank[:], lhsT=ones[:, 0:P], rhs=ones[:], start=True, stop=True
-                    )
-
-            idle_matmuls(WARM_UP)
-            for u in range(WIN_PER_SIDE):
-                means(u)
-                x_head = psum_head.tile([P, HALVES, PACK, P], BF16, name="head_bank")
-                tokens_to_partitions(u, x_head)
-            bias_bank = psum_head.tile([P, OUT_COLS], F32, name="head_bank")
-            spread_bias(0, bias_bank)
-            group_weight(0)
-            for u in range(WIN_PER_SIDE + 1):
-                if u == 2:
-                    quantise_weight(0)
-                    nc.vector.tensor_copy(out=gain[:], in_=gain_bf[:])
-                    nc.vector.tensor_copy(out=shift[:], in_=shift_bf[:])
-                if u < WIN_PER_SIDE:
-                    squares_and_std(u)
-                    reciprocal_std(u)
-                    normalise(u)
-                if u == WIN_PER_SIDE:
-                    gain_and_shift(0)
-                    regroup(0)
-                if u >= 1:
-                    low_head = psum_head.tile([P, 2, HALVES, P], F32, name="head_bank")
-                    high_head = psum_head.tile([P, 2, HALVES, P], F32, name="head_bank")
-                    channels_to_partitions(u - 1, low_head, high_head)
-                    idle_matmuls(KEEP_WARM)
-            means(WIN_PER_SIDE)
-            gain_and_shift(1)
-            regroup(1)
-            gain_and_shift(3)
-            gain_and_shift(2)
-            regroup(2)
-            regroup(3)
-
-        psum_x = ctx.enter_context(tc.psum_pool(name="psum_x", bufs=2))
-        psum_y = ctx.enter_context(tc.psum_pool(name="psum_y", bufs=1))
-        psum_acc = ctx.enter_context(tc.psum_pool(name="psum_acc", bufs=3))
 
         def project(b, o, sj):
             if sj == 0:
                 result = results.tile([P, HEADS, WIN, HEAD_DIM], F32)
                 result_of[o] = result
-            acc = psum_acc.tile([P, OUT_COLS], F32)
+            acc = next_acc([P, OUT_COLS])
             nc.tensor.matmul_mx(
                 out=acc[:],
                 lhsT=x_codes_of[b][:, sj * P : (sj + 1) * P].bitcast(FP8X4),
@@ -396,7 +373,7 @@ def tile_functatransformer_pa_t_kernel(
                 out=result_of[o][:, :, sj, :],
                 in0=acc[:].rearrange("p (h d) -> p h d", d=HEAD_DIM),
                 scalar=out_scales[o],
-                in1=bias_f32[o][:].rearrange("p (h d) -> p h d", d=HEAD_DIM),
+                in1=bias_of[o][:].rearrange("p (h d) -> p h d", d=HEAD_DIM),
                 op0=ALU.mult,
                 op1=ALU.add,
             )
@@ -407,51 +384,121 @@ def tile_functatransformer_pa_t_kernel(
                         in_=result_of[o][:, h].rearrange("p sj d -> p (sj d)"),
                     )
 
-        passes_of_step = {}
-        for number in range(PASSES):
-            passes_of_step.setdefault(WIN_PER_SIDE + number // 5, []).append((0, number))
-        for b in range(1, BATCH):
-            for number in range(PASSES):
-                step = WIN_PER_SIDE * b + LAG + number // PASSES_PER_STEP
-                passes_of_step.setdefault(step, []).append((b, number))
-
-        def project_some(k, part):
-            mine = passes_of_step.get(k, [])
-            cut = (len(mine) + 1) // 2
-            for b, number in mine[:cut] if part == 0 else mine[cut:]:
-                project(b, number // WIN, number % WIN)
-
-        x_t = psum_x.tile([P, HALVES, PACK, P], BF16)
-        tokens_to_partitions(WIN_PER_SIDE, x_t)
-        quantise_image(0)
+        idle_bank = bank(Y_BANKS[0], [P, OUT_COLS], F32)
+        for n in range(WARM_UP):
+            nc.tensor.matmul(
+                out=idle_bank[:], lhsT=ones[:, 0:P], rhs=ones[:], start=True, stop=True
+            )
+        low, high = (0, 1), (2, 3)
+        head_sums = bank(SUM_BANK, [P, 2 * WIN_PER_SIDE, HALVES, SUM_COLS], F32)
+        for u in range(3):
+            sums((u,), head_sums, u)
+            tokens_to_partitions(u)
+            negate_means((u,), head_sums, u)
+            if u == 0:
+                nc.vector.tensor_copy(out=gain[:], in_=gain_bf[:])
+                nc.vector.tensor_copy(out=shift[:], in_=shift_bf[:])
+        sums((3,), head_sums, 3)
+        group_weight(0)
+        squares_and_std(0)
+        reciprocal_std(0)
+        normalise(0)
+        tokens_to_partitions(3)
+        negate_means((3,), head_sums, 3)
+        squares_and_std(1)
+        reciprocal_std(1)
+        normalise(1)
+        channels_to_partitions(0)
+        squares_and_std(2)
+        reciprocal_std(2)
+        normalise(2)
+        channels_to_partitions(1)
+        squares_and_std(3)
+        second = range(WIN_PER_SIDE, 2 * WIN_PER_SIDE)
+        sums(second, head_sums, WIN_PER_SIDE)
+        negate_means(second, head_sums, WIN_PER_SIDE)
+        reciprocal_std(3)
+        normalise(3)
+        gain_and_shift(0, low + high, on_vector=False)
+        regroup(0, 0, "gpsimd")
+        channels_to_partitions(2)
+        gain_and_shift(1, low + high, on_vector=False)
+        regroup(1, 0, "gpsimd")
+        channels_to_partitions(3)
+        gain_and_shift(2, low, on_vector=False)
+        gain_and_shift(2, high, on_vector=True)
+        regroup(2, 0, "gpsimd")
+        scale_bias(0)
+        tokens_to_partitions(4)
+        quantise_weight(0)
+        gain_and_shift(3, low, on_vector=False)
+        gain_and_shift(3, high, on_vector=True)
+        regroup(3, 0, "vector")
+        quantise_half(0, 0)
+        regroup(3, 1, "vector")
+        for u in range(3):
+            regroup(u, 1, "gpsimd")
         group_weight(1)
         group_weight(2)
-        for k in range(WIN_PER_SIDE, UNITS + LAG):
+        squares_and_std(4)
+        tokens_to_partitions(5)
+
+        passes_of_step = {}
+        for step, first, end in ((4, 0, 8), (5, 8, 14), (6, 14, 19), (7, 19, 22), (8, 22, 24)):
+            passes_of_step[step] = [(0, number) for number in range(first, end)]
+        for b in range(1, BATCH):
+            for number in range(PASSES):
+                step = WIN_PER_SIDE * (b + 1) + 1 + number // (PASSES // WIN_PER_SIDE)
+                passes_of_step.setdefault(step, []).append((b, number))
+
+        passes_done = []
+
+        def project_some(mine):
+            for b, number in mine:
+                project(b, number // WIN, number % WIN)
+                passes_done.append(number)
+                if len(passes_done) == 1:
+                    reciprocal_std(WIN_PER_SIDE)
+                    normalise(WIN_PER_SIDE)
+                if len(passes_done) == 3:
+                    quantise_half(0, 1)
+                if len(passes_done) == WIN - 2:
+                    quantise_weight(1)
+                if len(passes_done) == 2 * WIN - 2:
+                    quantise_weight(2)
+                if number == WIN and b + 2 < BATCH:
+                    units = range(WIN_PER_SIDE * (b + 2), WIN_PER_SIDE * (b + 3))
+                    later_sums = next_acc([P, WIN_PER_SIDE, HALVES, SUM_COLS])
+                    sums(units, later_sums, 0)
+                    negate_means(units, later_sums, 0)
+
+        for k in range(WIN_PER_SIDE, UNITS + WIN_PER_SIDE + 1):
             behind = WIN_PER_SIDE <= k - 1 < UNITS
+            last_of_image = behind and k % WIN_PER_SIDE == 0
+            mine = passes_of_step.get(k, [])
+            cut = len(mine) // 2
             if behind:
-                y_t_low = psum_y.tile([P, 2, HALVES, P], F32)
-                y_t_high = psum_y.tile([P, 2, HALVES, P], F32)
-                channels_to_partitions(k - 1, y_t_low, y_t_high)
+                channels_to_partitions(k - 1)
             if k + 1 < UNITS:
-                means(k + 1)
-            if k < UNITS:
-                squares_and_std(k)
+                squares_and_std(k + 1)
             if behind:
-                gain_and_shift(k - 1)
-            if k < UNITS:
-                reciprocal_std(k)
+                gain_and_shift(k - 1, low, on_vector=False)
+                if not last_of_image:
+                    gain_and_shift(k - 1, high, on_vector=False)
+            if behind and k < UNITS:
                 normalise(k)
-            project_some(k, 0)
-            if k - WIN_PER_SIDE in (0, 1):
-                acc = psum_acc.tile([P, OUT_COLS], F32)
-                spread_bias(k - WIN_PER_SIDE + 1, acc)
+            project_some(mine[:cut])
             if k + 1 < UNITS:
-                x_t = psum_x.tile([P, HALVES, PACK, P], BF16)
-                tokens_to_partitions(k + 1, x_t)
-            project_some(k, 1)
-            if k - WIN_PER_SIDE in (0, 1):
-                quantise_weight(k - WIN_PER_SIDE + 1)
+                reciprocal_std(k + 1)
+            if last_of_image:
+                gain_and_shift(k - 1, high, on_vector=True)
+            if k + 2 < UNITS:
+                tokens_to_partitions(k + 2)
+            project_some(mine[cut:])
             if behind:
-                regroup(k - 1)
-                if k % WIN_PER_SIDE == 0:
-                    quantise_image(k // WIN_PER_SIDE - 1)
+                engine = "vector" if last_of_image else "gpsimd"
+                regroup(k - 1, 0, engine)
+                regroup(k - 1, 1, engine)
+                if last_of_image:
+                    quantise_half(k // WIN_PER_SIDE - 1, 0)
+                    quantise_half(k // WIN_PER_SIDE - 1, 1)

@@ -85,14 +85,14 @@ def tile_functatransformer_pa_t_kernel(
         x_view = [x[b].rearrange("(p t) i j -> p t (i j)", t=PACK) for b in range(BATCH)]
         piece_bounds = ((P, 2 * P), (3 * P, 2 * P), (5 * P, 3 * P), (0, P))
         pieces = []
-        for n, (first, count) in enumerate(piece_bounds):
+        def load_piece(n):
+            first, count = piece_bounds[n]
             piece = const.tile([P, PACK, count], BF16, name="piece%d" % n)
             nc.sync.dma_start(out=piece[:], in_=x_view[0][:, :, first : first + count])
             pieces.append(piece)
+
         gain_bf = const.tile([P, PACK], BF16)
         shift_bf = const.tile([P, PACK], BF16)
-        nc.sync.dma_start(out=gain_bf[:], in_=ln1_g.rearrange("(p t) -> p t", t=PACK))
-        nc.sync.dma_start(out=shift_bf[:], in_=ln1_b.rearrange("(p t) -> p t", t=PACK))
         w_raw = []
         x_tiles = [None]
         bias_of = []
@@ -112,13 +112,20 @@ def tile_functatransformer_pa_t_kernel(
             nc.sync.dma_start(out=bias_bf[:], in_=biases[o].partition_broadcast(P))
             bias_of.append(bias_bf)
 
+        load_piece(0)
         load_weight(0)
-        load_image(1)
-        for o in range(3):
-            load_bias(o)
+        load_piece(1)
+        load_piece(2)
+        load_piece(3)
         load_weight(1)
+        nc.sync.dma_start(out=gain_bf[:], in_=ln1_g.rearrange("(p t) -> p t", t=PACK))
+        nc.sync.dma_start(out=shift_bf[:], in_=ln1_b.rearrange("(p t) -> p t", t=PACK))
+        load_image(1)
         load_weight(2)
+        load_bias(0)
+        load_bias(1)
         load_image(2)
+        load_bias(2)
         load_image(3)
 
         warm = const.tile([P, 1], F32)
@@ -143,15 +150,20 @@ def tile_functatransformer_pa_t_kernel(
             gpsimd_move(scaled[:], bias_of[o][:], factor=out_scales[o])
             bias_of[o] = scaled
 
-        def group_weight(o):
-            w_grouped = wstage.tile([P, OUT_COLS, PACK], BF16, align_bytes=64)
+        def group_weight(o, parts, on_vector=False):
+            if o not in w_grouped_of:
+                w_grouped = wstage.tile([P, OUT_COLS, PACK], BF16, align_bytes=64)
+                w_grouped_of[o] = w_grouped
             side_by_side = w_raw[o][:].rearrange("p t n -> p n t")
-            for first in range(0, OUT_COLS, GPSIMD_COLS):
-                gpsimd_move(
-                    w_grouped[:, first : first + GPSIMD_COLS, :],
-                    side_by_side[:, first : first + GPSIMD_COLS, :],
+            if on_vector:
+                cols = slice(parts[0] * GPSIMD_COLS, (parts[-1] + 1) * GPSIMD_COLS)
+                nc.vector.tensor_copy(
+                    out=w_grouped_of[o][:, cols, :], in_=side_by_side[:, cols, :]
                 )
-            w_grouped_of[o] = w_grouped
+                return
+            for part in parts:
+                cols = slice(part * GPSIMD_COLS, (part + 1) * GPSIMD_COLS)
+                gpsimd_move(w_grouped_of[o][:, cols, :], side_by_side[:, cols, :])
 
         def quantise_weight(o):
             codes = const.tile([P, OUT_COLS], U32, align_bytes=64, name="w_codes%d" % o)
@@ -395,12 +407,11 @@ def tile_functatransformer_pa_t_kernel(
             sums((u,), head_sums, u)
             tokens_to_partitions(u)
             negate_means((u,), head_sums, u)
-            if u == 0:
-                nc.vector.tensor_copy(out=gain[:], in_=gain_bf[:])
-                nc.vector.tensor_copy(out=shift[:], in_=shift_bf[:])
+            if u < 2:
+                group_weight(0, (2 * u, 2 * u + 1), on_vector=True)
         sums((3,), head_sums, 3)
-        group_weight(0)
         squares_and_std(0)
+        group_weight(1, (0, 1, 2))
         reciprocal_std(0)
         normalise(0)
         tokens_to_partitions(3)
@@ -408,6 +419,8 @@ def tile_functatransformer_pa_t_kernel(
         squares_and_std(1)
         reciprocal_std(1)
         normalise(1)
+        nc.vector.tensor_copy(out=gain[:], in_=gain_bf[:])
+        nc.vector.tensor_copy(out=shift[:], in_=shift_bf[:])
         channels_to_partitions(0)
         squares_and_std(2)
         reciprocal_std(2)
@@ -428,18 +441,18 @@ def tile_functatransformer_pa_t_kernel(
         gain_and_shift(2, low, on_vector=False)
         gain_and_shift(2, high, on_vector=True)
         regroup(2, 0, "gpsimd")
+        quantise_weight(0)
         scale_bias(0)
         tokens_to_partitions(4)
-        quantise_weight(0)
         gain_and_shift(3, low, on_vector=False)
         gain_and_shift(3, high, on_vector=True)
         regroup(3, 0, "vector")
         quantise_half(0, 0)
         regroup(3, 1, "vector")
         for u in range(3):
-            regroup(u, 1, "gpsimd")
-        group_weight(1)
-        group_weight(2)
+            regroup(u, 1, "vector" if u == 2 else "gpsimd")
+        group_weight(1, (3,))
+        group_weight(2, (0, 1, 2, 3))
         squares_and_std(4)
         tokens_to_partitions(5)
 

@@ -238,7 +238,7 @@ def tile_functatransformer_pa_t_kernel(
             x_t = bank(number, [P, HALVES, PACK, P], BF16)
             for half in range(HALVES):
                 for t in range(PACK):
-                    if u <= WIN_PER_SIDE:
+                    if u <= 12:
                         nc.tensor.matmul(
                             out=x_t[:, half, t, :], lhsT=x_block(u, half, t), rhs=ident_bf[:],
                             start=True, stop=True,
@@ -367,7 +367,7 @@ def tile_functatransformer_pa_t_kernel(
                 ),
             )
 
-        def project(b, o, sj):
+        def project(b, o, sj, shared=False):
             if sj == 0:
                 result = results.tile([P, HEADS, WIN, HEAD_DIM], F32)
                 result_of[o] = result
@@ -381,14 +381,17 @@ def tile_functatransformer_pa_t_kernel(
                 start=True,
                 stop=True,
             )
-            nc.vector.scalar_tensor_tensor(
-                out=result_of[o][:, :, sj, :],
-                in0=acc[:].rearrange("p (h d) -> p h d", d=HEAD_DIM),
-                scalar=out_scales[o],
-                in1=bias_of[o][:].rearrange("p (h d) -> p h d", d=HEAD_DIM),
-                op0=ALU.mult,
-                op1=ALU.add,
-            )
+            mine = result_of[o][:, :, sj, :]
+            sums_in = acc[:].rearrange("p (h d) -> p h d", d=HEAD_DIM)
+            bias_in = bias_of[o][:].rearrange("p (h d) -> p h d", d=HEAD_DIM)
+            if shared:
+                nc.scalar.activation(out=mine, in_=sums_in, func=ACT.Copy, scale=out_scales[o])
+                nc.gpsimd.tensor_tensor(out=mine, in0=mine, in1=bias_in, op=ALU.add)
+            else:
+                nc.vector.scalar_tensor_tensor(
+                    out=mine, in0=sums_in, scalar=out_scales[o], in1=bias_in,
+                    op0=ALU.mult, op1=ALU.add,
+                )
             if sj == WIN - 1:
                 for h in range(HEADS):
                     nc.sync.dma_start(
@@ -468,7 +471,8 @@ def tile_functatransformer_pa_t_kernel(
 
         def project_some(mine):
             for b, number in mine:
-                project(b, number // WIN, number % WIN)
+                shared = b == BATCH - 1 and number % 4 == 1
+                project(b, number // WIN, number % WIN, shared)
                 passes_done.append(number)
                 if len(passes_done) == 1:
                     reciprocal_std(WIN_PER_SIDE)
@@ -495,16 +499,14 @@ def tile_functatransformer_pa_t_kernel(
             if k + 1 < UNITS:
                 squares_and_std(k + 1)
             if behind:
-                gain_and_shift(k - 1, low, on_vector=False)
-                if not last_of_image:
-                    gain_and_shift(k - 1, high, on_vector=False)
+                gain_and_shift(k - 1, low + high[:1], on_vector=False)
             if behind and k < UNITS:
                 normalise(k)
             project_some(mine[:cut])
             if k + 1 < UNITS:
                 reciprocal_std(k + 1)
-            if last_of_image:
-                gain_and_shift(k - 1, high, on_vector=True)
+            if behind:
+                gain_and_shift(k - 1, high[1:], on_vector=True)
             if k + 2 < UNITS:
                 tokens_to_partitions(k + 2)
             project_some(mine[cut:])

@@ -187,6 +187,7 @@ def tile_functatransformer_pa_t_kernel(
 
         neg_mean_of = {}
         x_t_of = {}
+        sum_sq_of = {}
         std_of = {}
         rstd_of = {}
         neg_mean_rstd_of = {}
@@ -250,21 +251,25 @@ def tile_functatransformer_pa_t_kernel(
                         )
             x_t_of[u] = x_t
 
-        def squares_and_std(u):
+        def squares(u):
             sum_sq = stats.tile([P, HALVES], F32)
+            sum_sq_of[u] = sum_sq
             for half in range(HALVES):
-                squares = norm.tile([P, CHANNELS], BF16)
+                squared = norm.tile([P, CHANNELS], BF16)
                 nc.scalar.activation(
-                    out=squares[:],
+                    out=squared[:],
                     in_=x_t_of[u][:, half].rearrange("p t c -> p (t c)"),
                     func=ACT.Square,
                     bias=neg_mean_of[u][:, half : half + 1],
                     scale=1.0,
                     accum_out=sum_sq[:, half : half + 1],
                 )
+
+        def root(u):
             std = stats.tile([P, HALVES], F32)
             nc.scalar.activation(
-                out=std[:], in_=sum_sq[:], func=ACT.Sqrt, bias=eps[:, 0:1], scale=1.0 / CHANNELS
+                out=std[:], in_=sum_sq_of[u][:], func=ACT.Sqrt, bias=eps[:, 0:1],
+                scale=1.0 / CHANNELS,
             )
             std_of[u] = std
 
@@ -272,12 +277,13 @@ def tile_functatransformer_pa_t_kernel(
             rstd = stats.tile([P, HALVES], F32)
             nc.vector.reciprocal(out=rstd[:], in_=std_of[u][:])
             rstd_of[u] = rstd
-            if u >= WIN_PER_SIDE:
-                neg_mean_rstd = stats.tile([P, HALVES], F32)
-                nc.vector.tensor_tensor(
-                    out=neg_mean_rstd[:], in0=neg_mean_of[u], in1=rstd[:], op=ALU.mult
-                )
-                neg_mean_rstd_of[u] = neg_mean_rstd
+
+        def product(u):
+            neg_mean_rstd = stats.tile([P, HALVES], F32)
+            nc.vector.tensor_tensor(
+                out=neg_mean_rstd[:], in0=neg_mean_of[u], in1=rstd_of[u][:], op=ALU.mult
+            )
+            neg_mean_rstd_of[u] = neg_mean_rstd
 
         def normalise(u):
             y_of[u] = []
@@ -413,23 +419,27 @@ def tile_functatransformer_pa_t_kernel(
             if u < 2:
                 group_weight(0, (2 * u, 2 * u + 1), on_vector=True)
         sums((3,), head_sums, 3)
-        squares_and_std(0)
+        squares(0)
+        root(0)
         group_weight(1, (0, 1, 2))
         reciprocal_std(0)
         normalise(0)
         tokens_to_partitions(3)
         negate_means((3,), head_sums, 3)
-        squares_and_std(1)
+        squares(1)
+        root(1)
         reciprocal_std(1)
         normalise(1)
         nc.vector.tensor_copy(out=gain[:], in_=gain_bf[:])
         nc.vector.tensor_copy(out=shift[:], in_=shift_bf[:])
         channels_to_partitions(0)
-        squares_and_std(2)
+        squares(2)
+        root(2)
         reciprocal_std(2)
         normalise(2)
         channels_to_partitions(1)
-        squares_and_std(3)
+        squares(3)
+        root(3)
         second = range(WIN_PER_SIDE, 2 * WIN_PER_SIDE)
         sums(second, head_sums, WIN_PER_SIDE)
         negate_means(second, head_sums, WIN_PER_SIDE)
@@ -456,7 +466,8 @@ def tile_functatransformer_pa_t_kernel(
             regroup(u, 1, "vector" if u == 2 else "gpsimd")
         group_weight(1, (3,))
         group_weight(2, (0, 1, 2, 3))
-        squares_and_std(4)
+        squares(4)
+        root(4)
         tokens_to_partitions(5)
 
         passes_of_step = {}
@@ -476,6 +487,8 @@ def tile_functatransformer_pa_t_kernel(
                 passes_done.append(number)
                 if len(passes_done) == 1:
                     reciprocal_std(WIN_PER_SIDE)
+                if len(passes_done) == 2:
+                    product(WIN_PER_SIDE)
                     normalise(WIN_PER_SIDE)
                 if len(passes_done) == 3:
                     quantise_half(0, 1)
@@ -497,9 +510,13 @@ def tile_functatransformer_pa_t_kernel(
             if behind:
                 channels_to_partitions(k - 1)
             if k + 1 < UNITS:
-                squares_and_std(k + 1)
+                squares(k + 1)
             if behind:
-                gain_and_shift(k - 1, low + high[:1], on_vector=False)
+                gain_and_shift(k - 1, low[:1], on_vector=False)
+            if k + 1 < UNITS:
+                root(k + 1)
+            if behind:
+                gain_and_shift(k - 1, low[1:] + high[:1], on_vector=False)
             if behind and k < UNITS:
                 normalise(k)
             project_some(mine[:cut])
@@ -509,7 +526,10 @@ def tile_functatransformer_pa_t_kernel(
                 gain_and_shift(k - 1, high[1:], on_vector=True)
             if k + 2 < UNITS:
                 tokens_to_partitions(k + 2)
-            project_some(mine[cut:])
+            project_some(mine[cut : cut + 1])
+            if k + 1 < UNITS:
+                product(k + 1)
+            project_some(mine[cut + 1 :])
             if behind:
                 engine = "vector" if last_of_image else "gpsimd"
                 regroup(k - 1, 0, engine)

@@ -440,9 +440,7 @@ def tile_functatransformer_pa_t_kernel(
         channels_to_partitions(1)
         squares(3)
         root(3)
-        second = range(WIN_PER_SIDE, 2 * WIN_PER_SIDE)
-        sums(second, head_sums, WIN_PER_SIDE)
-        negate_means(second, head_sums, WIN_PER_SIDE)
+        sums((4, 5), head_sums, 4)
         reciprocal_std(3)
         normalise(3)
         gain_and_shift(0, low + high, on_vector=False)
@@ -454,6 +452,7 @@ def tile_functatransformer_pa_t_kernel(
         gain_and_shift(2, low, on_vector=False)
         gain_and_shift(2, high, on_vector=True)
         regroup(2, 0, "gpsimd")
+        negate_means((4, 5), head_sums, 4)
         quantise_weight(0)
         scale_bias(0)
         tokens_to_partitions(4)
@@ -469,9 +468,12 @@ def tile_functatransformer_pa_t_kernel(
         squares(4)
         root(4)
         tokens_to_partitions(5)
+        sums((6, 7), head_sums, 6)
+        reciprocal_std(4)
+        negate_means((6, 7), head_sums, 6)
 
         passes_of_step = {}
-        for step, first, end in ((4, 0, 8), (5, 8, 14), (6, 14, 19), (7, 19, 22), (8, 22, 24)):
+        for step, first, end in ((4, 0, 6), (5, 6, 12), (6, 12, 18), (7, 18, 22), (8, 22, 24)):
             passes_of_step[step] = [(0, number) for number in range(first, end)]
         for b in range(1, BATCH):
             for number in range(PASSES):
@@ -479,15 +481,14 @@ def tile_functatransformer_pa_t_kernel(
                 passes_of_step.setdefault(step, []).append((b, number))
 
         passes_done = []
+        later_sums = {}
 
         def project_some(mine):
             for b, number in mine:
-                shared = b == BATCH - 1 and number % 4 == 1
+                shared = (b == BATCH - 1 and number % 4 == 1 or b in (1, 2) and number % 6 == 3)
                 project(b, number // WIN, number % WIN, shared)
                 passes_done.append(number)
                 if len(passes_done) == 1:
-                    reciprocal_std(WIN_PER_SIDE)
-                if len(passes_done) == 2:
                     product(WIN_PER_SIDE)
                     normalise(WIN_PER_SIDE)
                 if len(passes_done) == 3:
@@ -496,11 +497,12 @@ def tile_functatransformer_pa_t_kernel(
                     quantise_weight(1)
                 if len(passes_done) == 2 * WIN - 2:
                     quantise_weight(2)
-                if number == WIN and b + 2 < BATCH:
-                    units = range(WIN_PER_SIDE * (b + 2), WIN_PER_SIDE * (b + 3))
-                    later_sums = next_acc([P, WIN_PER_SIDE, HALVES, SUM_COLS])
-                    sums(units, later_sums, 0)
-                    negate_means(units, later_sums, 0)
+                first = WIN_PER_SIDE * (b + 2) + (0 if number < 13 else 2)
+                if number in (7, 13) and b + 2 < BATCH:
+                    later_sums[b] = next_acc([P, 2, HALVES, SUM_COLS])
+                    sums((first, first + 1), later_sums[b], 0)
+                if number - 1 in (7, 13) and b + 2 < BATCH:
+                    negate_means((first, first + 1), later_sums[b], 0)
 
         for k in range(WIN_PER_SIDE, UNITS + WIN_PER_SIDE + 1):
             behind = WIN_PER_SIDE <= k - 1 < UNITS

from contextlib import ExitStack

import concourse.mybir as mybir
from concourse.masks import make_identity

BF16 = mybir.dt.bfloat16
F32 = mybir.dt.float32
U32 = mybir.dt.uint32
U8 = mybir.dt.uint8
FP8X4 = mybir.dt.float8_e4m3fn_x4
ACT = mybir.ActivationFunctionType
ALU = mybir.AluOpType

P = 128
PACK = 4
BATCH = 4
CHANNELS = P * PACK
SIDE = 32
TOKENS = SIDE * SIDE
WIN = 8
SHIFT = WIN // 2
WIN_PER_SIDE = SIDE // WIN
HEADS = 16
HEAD_DIM = 32
OUT_COLS = HEADS * HEAD_DIM
EPS = 1e-5
TILE_ROWS = P // SIDE
TILES = TOKENS // P
HALVES = WIN // TILE_ROWS
SUM_COLS = 8
UNITS = BATCH * WIN_PER_SIDE
PASSES = 3 * WIN
WARM_UP = 3
HEAD_X_BANKS = (0, 1, 2, 0)
X_BANKS = (0, 1, 2)
HEAD_Y_BANKS = ((3, 4), (5, 6), (3, 4), (1, 2))
Y_BANKS = (3, 4)
ACC_BANKS = (5, 6, 7)
SUM_BANK = 7
GPSIMD_COLS = 128

FLOPS = 2 * BATCH * TOKENS * CHANNELS * 3 * OUT_COLS


def build_token_sort(nc, const):
    ident_f32 = const.tile([P, P], F32)
    make_identity(nc, ident_f32[:])
    ident_rows = ident_f32[:].rearrange("p (r j) -> p r j", j=SIDE)
    shifted = const.tile([P, TILE_ROWS, SIDE], F32)
    nc.vector.tensor_copy(out=shifted[:, :, 0 : SIDE - SHIFT], in_=ident_rows[:, :, SHIFT:SIDE])
    nc.vector.tensor_copy(out=shifted[:, :, SIDE - SHIFT : SIDE], in_=ident_rows[:, :, 0:SHIFT])
    token_sort = const.tile([P, P], F32)
    nc.vector.tensor_copy(
        out=token_sort[:].rearrange("p (sj wj r) -> p sj wj r", sj=WIN, r=TILE_ROWS),
        in_=shifted[:].rearrange("p r (wj sj) -> p sj wj r", sj=WIN),
    )
    return token_sort


def tile_functatransformer_pa_t_kernel(
    tc, x, ln1_g, ln1_b, Wq, bq, Wk, bk, Wv, bv, out_0, out_1, out_2
):
    nc = tc.nc
    weights = (Wq, Wk, Wv)
    biases = (bq, bk, bv)
    outs = (out_0, out_1, out_2)
    out_scales = (HEAD_DIM**-0.5, 1.0, 1.0)

    with ExitStack() as ctx:
        const = ctx.enter_context(tc.tile_pool(name="const", bufs=1))
        images = ctx.enter_context(tc.tile_pool(name="images", bufs=BATCH - 1))
        wstage = ctx.enter_context(tc.tile_pool(name="wstage", bufs=3))
        stats = ctx.enter_context(tc.tile_pool(name="stats", bufs=6))
        norm = ctx.enter_context(tc.tile_pool(name="norm", bufs=4))
        quant = ctx.enter_context(tc.tile_pool(name="quant", bufs=2))
        results = ctx.enter_context(tc.tile_pool(name="results", bufs=4))
        psum = ctx.enter_context(tc.psum_pool(name="psum", bufs=1))
        ctx.enter_context(tc.manual_schedule())

        ones = const.tile([P, OUT_COLS], BF16)
        nc.vector.memset(ones[:], 1.0)
        eps = const.tile([P, 1], F32)
        nc.vector.memset(eps[:], EPS)

        x_view = [x[b].rearrange("(p t) i j -> p t (i j)", t=PACK) for b in range(BATCH)]
        piece_bounds = ((P, 2 * P), (3 * P, 2 * P), (5 * P, 3 * P), (0, P))
        pieces = []
        def load_piece(n):
            first, count = piece_bounds[n]
            piece = const.tile([P, PACK, count], BF16, name="piece%d" % n)
            nc.sync.dma_start(out=piece[:], in_=x_view[0][:, :, first : first + count])
            pieces.append(piece)

        gain_bf = const.tile([P, PACK], BF16)
        shift_bf = const.tile([P, PACK], BF16)
        w_raw = []
        x_tiles = [None]
        bias_of = []

        def load_weight(o):
            raw = wstage.tile([P, PACK, OUT_COLS], BF16, name="w_raw")
            nc.sync.dma_start(out=raw[:], in_=weights[o].rearrange("(p t) n -> p t n", t=PACK))
            w_raw.append(raw)

        def load_image(b):
            x_sb = images.tile([P, PACK, TOKENS], BF16, name="x_sb")
            nc.sync.dma_start(out=x_sb[:], in_=x_view[b])
            x_tiles.append(x_sb)

        def load_bias(o):
            bias_bf = const.tile([P, OUT_COLS], BF16, name="bias_bf%d" % o)
            nc.sync.dma_start(out=bias_bf[:], in_=biases[o].partition_broadcast(P))
            bias_of.append(bias_bf)

        load_piece(0)
        load_weight(0)
        load_piece(1)
        load_piece(2)
        load_piece(3)
        load_weight(1)
        nc.sync.dma_start(out=gain_bf[:], in_=ln1_g.rearrange("(p t) -> p t", t=PACK))
        nc.sync.dma_start(out=shift_bf[:], in_=ln1_b.rearrange("(p t) -> p t", t=PACK))
        load_image(1)
        load_weight(2)
        load_bias(0)
        load_bias(1)
        load_image(2)
        load_bias(2)
        load_image(3)

        warm = const.tile([P, 1], F32)
        nc.scalar.activation(out=warm[:], in_=eps[:], func=ACT.Sqrt)
        ident_bf = const.tile([P, P], BF16)
        make_identity(nc, ident_bf[:])
        token_sort = build_token_sort(nc, const)
        gain = const.tile([P, PACK], F32)
        shift = const.tile([P, PACK], F32)

        w_grouped_of = {}
        w_codes = {}
        w_scales = {}

        def gpsimd_move(out, in_, factor=1.0):
            nc.gpsimd.tensor_scalar(
                out=out, in0=in_, scalar1=factor, scalar2=0.0, op0=ALU.mult, op1=ALU.add
            )

        def scale_bias(o):
            scaled = const.tile([P, OUT_COLS], F32, name="bias_scaled")
            gpsimd_move(scaled[:], bias_of[o][:], factor=out_scales[o])
            bias_of[o] = scaled

        def group_weight(o, parts, on_vector=False):
            if o not in w_grouped_of:
                w_grouped = wstage.tile([P, OUT_COLS, PACK], BF16, align_bytes=64)
                w_grouped_of[o] = w_grouped
            side_by_side = w_raw[o][:].rearrange("p t n -> p n t")
            if on_vector:
                cols = slice(parts[0] * GPSIMD_COLS, (parts[-1] + 1) * GPSIMD_COLS)
                nc.vector.tensor_copy(
                    out=w_grouped_of[o][:, cols, :], in_=side_by_side[:, cols, :]
                )
                return
            for part in parts:
                cols = slice(part * GPSIMD_COLS, (part + 1) * GPSIMD_COLS)
                gpsimd_move(w_grouped_of[o][:, cols, :], side_by_side[:, cols, :])

        def quantise_weight(o):
            codes = const.tile([P, OUT_COLS], U32, align_bytes=64, name="w_codes%d" % o)
            scales = const.tile([P, OUT_COLS], U8, align_bytes=64, name="w_scales%d" % o)
            nc.vector.quantize_mx(
                out=codes[:].bitcast(FP8X4),
                scales=scales[:],
                in_=w_grouped_of[o][:].rearrange("p n t -> p (n t)"),
            )
            w_codes[o] = codes
            w_scales[o] = scales

        def bank(number, shape, dtype):
            return psum.tile(shape, dtype, name="bank%d" % number)

        acc_count = []

        def next_acc(shape):
            acc_count.append(None)
            return bank(ACC_BANKS[(len(acc_count) - 1) % len(ACC_BANKS)], shape, F32)

        neg_mean_of = {}
        x_t_of = {}
        sum_sq_of = {}
        std_of = {}
        rstd_of = {}
        neg_mean_rstd_of = {}
        y_of = {}
        y_t_of = {}
        planes_of = {}
        grouped_of = {}
        x_codes_of = {}
        x_scales_of = {}
        result_of = {}

        def x_block(u, half, t):
            a = HALVES * (u % WIN_PER_SIDE) + half
            first = ((a + 1) % TILES) * P
            if u >= WIN_PER_SIDE:
                return x_tiles[u // WIN_PER_SIDE][:, t, first : first + P]
            for n, (start, count) in enumerate(piece_bounds):
                if start <= first < start + count:
                    return pieces[n][:, t, first - start : first - start + P]
            return None

        def sums(units, tile, place):
            for n, u in enumerate(units):
                for half in range(HALVES):
                    for t in range(PACK):
                        nc.tensor.matmul(
                            out=tile[:, place + n, half, :],
                            lhsT=x_block(u, half, t),
                            rhs=ones[:, 0:SUM_COLS],
                            start=(t == 0),
                            stop=(t == PACK - 1),
                        )

        def negate_means(units, tile, place):
            neg_mean = stats.tile([P, WIN_PER_SIDE, HALVES], F32)
            count = len(units)
            nc.vector.tensor_scalar(
                out=neg_mean[:, 0:count], in0=tile[:, place : place + count, :, 0],
                scalar1=-1.0 / CHANNELS, scalar2=None, op0=ALU.mult,
            )
            for n, u in enumerate(units):
                neg_mean_of[u] = neg_mean[:, n]

        def tokens_to_partitions(u):
            if u < WIN_PER_SIDE:
                number = HEAD_X_BANKS[u]
            else:
                number = X_BANKS[(u - WIN_PER_SIDE) % len(X_BANKS)]
            x_t = bank(number, [P, HALVES, PACK, P], BF16)
            for half in range(HALVES):
                for t in range(PACK):
                    if u <= 12:
                        nc.tensor.matmul(
                            out=x_t[:, half, t, :], lhsT=x_block(u, half, t), rhs=ident_bf[:],
                            start=True, stop=True,
                        )
                    else:
                        nc.tensor.transpose(
                            out=x_t[:, half, t, :], in_=x_block(u, half, t),
                            identity=ident_bf[:],
                        )
            x_t_of[u] = x_t

        def squares(u):
            sum_sq = stats.tile([P, HALVES], F32)
            sum_sq_of[u] = sum_sq
            for half in range(HALVES):
                squared = norm.tile([P, CHANNELS], BF16)
                nc.scalar.activation(
                    out=squared[:],
                    in_=x_t_of[u][:, half].rearrange("p t c -> p (t c)"),
                    func=ACT.Square,
                    bias=neg_mean_of[u][:, half : half + 1],
                    scale=1.0,
                    accum_out=sum_sq[:, half : half + 1],
                )

        def root(u):
            std = stats.tile([P, HALVES], F32)
            nc.scalar.activation(
                out=std[:], in_=sum_sq_of[u][:], func=ACT.Sqrt, bias=eps[:, 0:1],
                scale=1.0 / CHANNELS,
            )
            std_of[u] = std

        def reciprocal_std(u):
            rstd = stats.tile([P, HALVES], F32)
            nc.vector.reciprocal(out=rstd[:], in_=std_of[u][:])
            rstd_of[u] = rstd

        def product(u):
            neg_mean_rstd = stats.tile([P, HALVES], F32)
            nc.vector.tensor_tensor(
                out=neg_mean_rstd[:], in0=neg_mean_of[u], in1=rstd_of[u][:], op=ALU.mult
            )
            neg_mean_rstd_of[u] = neg_mean_rstd

        def normalise(u):
            y_of[u] = []
            for half in range(HALVES):
                y = norm.tile([P, PACK, P], F32)
                if u < WIN_PER_SIDE:
                    nc.vector.tensor_scalar(
                        out=y[:].rearrange("p t c -> p (t c)"),
                        in0=x_t_of[u][:, half].rearrange("p t c -> p (t c)"),
                        scalar1=neg_mean_of[u][:, half : half + 1],
                        scalar2=rstd_of[u][:, half : half + 1],
                        op0=ALU.add,
                        op1=ALU.mult,
                    )
                else:
                    nc.scalar.activation(
                        out=y[:].rearrange("p t c -> p (t c)"),
                        in_=x_t_of[u][:, half].rearrange("p t c -> p (t c)"),
                        func=ACT.Identity,
                        bias=neg_mean_rstd_of[u][:, half : half + 1],
                        scale=rstd_of[u][:, half : half + 1],
                    )
                y_of[u].append(y)

        def channels_to_partitions(u):
            numbers = HEAD_Y_BANKS[u] if u < WIN_PER_SIDE else Y_BANKS
            y_t_of[u] = [bank(number, [P, 2, HALVES, P], F32) for number in numbers]
            for t in range(PACK):
                for half in range(HALVES):
                    nc.tensor.transpose(
                        out=y_t_of[u][t // 2][:, t % 2, half, :],
                        in_=y_of[u][half][:, t, :],
                        identity=token_sort[:],
                    )

        def gain_and_shift(u, slots, on_vector):
            if u not in planes_of:
                planes = norm.tile([P, PACK, HALVES * P], BF16)
                planes_of[u] = planes
            for t in slots:
                sorted_out = planes_of[u][:, t, :].rearrange(
                    "p (g half r) -> p g half r", half=HALVES, r=TILE_ROWS
                )
                sorted_in = y_t_of[u][t // 2][:, t % 2].rearrange(
                    "p half (g r) -> p g half r", r=TILE_ROWS
                )
                if on_vector:
                    nc.vector.tensor_scalar(
                        out=sorted_out, in0=sorted_in, scalar1=gain[:, t : t + 1],
                        scalar2=shift[:, t : t + 1], op0=ALU.mult, op1=ALU.add,
                    )
                else:
                    nc.scalar.activation(
                        out=sorted_out, in_=sorted_in, func=ACT.Identity,
                        bias=shift[:, t : t + 1], scale=gain[:, t : t + 1],
                    )

        def regroup(u, part, engine):
            b = u // WIN_PER_SIDE
            wi = u % WIN_PER_SIDE
            if b not in grouped_of:
                grouped = quant.tile([P, WIN, P, PACK], BF16, align_bytes=64)
                grouped_of[b] = grouped
            per_row = WIN_PER_SIDE * WIN
            cols = slice(part * WIN // 2, (part + 1) * WIN // 2)
            mine = grouped_of[b][:, cols, per_row * wi : per_row * (wi + 1), :]
            side_by_side = planes_of[u][:].rearrange("p t (sj c) -> p sj c t", sj=WIN)[:, cols]
            if engine == "vector":
                nc.vector.tensor_copy(out=mine, in_=side_by_side)
            elif engine == "scalar":
                nc.scalar.copy(out=mine, in_=side_by_side)
            else:
                gpsimd_move(mine, side_by_side)

        def quantise_half(b, part):
            if part == 0:
                x_codes = quant.tile([P, WIN * P], U32, align_bytes=64)
                x_scales = quant.tile([P, WIN * P], U8, align_bytes=64)
                x_codes_of[b] = x_codes
                x_scales_of[b] = x_scales
            cols = slice(part * WIN // 2 * P, (part + 1) * WIN // 2 * P)
            nc.vector.quantize_mx(
                out=x_codes_of[b][:, cols].bitcast(FP8X4),
                scales=x_scales_of[b][:, cols],
                in_=grouped_of[b][:, part * WIN // 2 : (part + 1) * WIN // 2].rearrange(
                    "p sj m t -> p (sj m t)"
                ),
            )

        def project(b, o, sj, shared=False):
            if sj == 0:
                result = results.tile([P, HEADS, WIN, HEAD_DIM], F32)
                result_of[o] = result
            acc = next_acc([P, OUT_COLS])
            nc.tensor.matmul_mx(
                out=acc[:],
                lhsT=x_codes_of[b][:, sj * P : (sj + 1) * P].bitcast(FP8X4),
                lhsT_scale=x_scales_of[b][:, sj * P : (sj + 1) * P],
                rhs=w_codes[o][:].bitcast(FP8X4),
                rhs_scale=w_scales[o][:],
                start=True,
                stop=True,
            )
            mine = result_of[o][:, :, sj, :]
            sums_in = acc[:].rearrange("p (h d) -> p h d", d=HEAD_DIM)
            bias_in = bias_of[o][:].rearrange("p (h d) -> p h d", d=HEAD_DIM)
            if shared:
                nc.scalar.activation(out=mine, in_=sums_in, func=ACT.Copy, scale=out_scales[o])
                nc.gpsimd.tensor_tensor(out=mine, in0=mine, in1=bias_in, op=ALU.add)
            else:
                nc.vector.scalar_tensor_tensor(
                    out=mine, in0=sums_in, scalar=out_scales[o], in1=bias_in,
                    op0=ALU.mult, op1=ALU.add,
                )
            if sj == WIN - 1:
                for h in range(HEADS):
                    nc.sync.dma_start(
                        out=outs[o][b, :, h].rearrange("w (si sj) d -> w si (sj d)", sj=WIN),
                        in_=result_of[o][:, h].rearrange("p sj d -> p (sj d)"),
                    )

        idle_bank = bank(Y_BANKS[0], [P, OUT_COLS], F32)
        for n in range(WARM_UP):
            nc.tensor.matmul(
                out=idle_bank[:], lhsT=ones[:, 0:P], rhs=ones[:], start=True, stop=True
            )
        low, high = (0, 1), (2, 3)
        head_sums = bank(SUM_BANK, [P, 2 * WIN_PER_SIDE, HALVES, SUM_COLS], F32)
        for u in range(3):
            sums((u,), head_sums, u)
            tokens_to_partitions(u)
            negate_means((u,), head_sums, u)
            if u < 2:
                group_weight(0, (2 * u, 2 * u + 1), on_vector=True)
        sums((3,), head_sums, 3)
        squares(0)
        root(0)
        group_weight(1, (0, 1, 2))
        reciprocal_std(0)
        normalise(0)
        tokens_to_partitions(3)
        negate_means((3,), head_sums, 3)
        squares(1)
        root(1)
        reciprocal_std(1)
        normalise(1)
        nc.vector.tensor_copy(out=gain[:], in_=gain_bf[:])
        nc.vector.tensor_copy(out=shift[:], in_=shift_bf[:])
        channels_to_partitions(0)
        squares(2)
        root(2)
        reciprocal_std(2)
        normalise(2)
        channels_to_partitions(1)
        squares(3)
        root(3)
        sums((4, 5), head_sums, 4)
        reciprocal_std(3)
        normalise(3)
        gain_and_shift(0, low + high, on_vector=False)
        regroup(0, 0, "gpsimd")
        channels_to_partitions(2)
        gain_and_shift(1, low + high, on_vector=False)
        regroup(1, 0, "gpsimd")
        channels_to_partitions(3)
        gain_and_shift(2, low, on_vector=False)
        gain_and_shift(2, high, on_vector=True)
        regroup(2, 0, "gpsimd")
        negate_means((4, 5), head_sums, 4)
        quantise_weight(0)
        scale_bias(0)
        tokens_to_partitions(4)
        gain_and_shift(3, low, on_vector=False)
        gain_and_shift(3, high, on_vector=True)
        regroup(3, 0, "vector")
        quantise_half(0, 0)
        regroup(3, 1, "vector")
        for u in range(3):
            regroup(u, 1, "vector" if u == 2 else "gpsimd")
        group_weight(1, (3,))
        group_weight(2, (0, 1, 2, 3))
        squares(4)
        root(4)
        tokens_to_partitions(5)
        sums((6, 7), head_sums, 6)
        reciprocal_std(4)
        negate_means((6, 7), head_sums, 6)

        passes_of_step = {}
        for step, first, end in ((4, 0, 6), (5, 6, 12), (6, 12, 18), (7, 18, 22), (8, 22, 24)):
            passes_of_step[step] = [(0, number) for number in range(first, end)]
        for b in range(1, BATCH):
            for number in range(PASSES):
                step = WIN_PER_SIDE * (b + 1) + 1 + number // (PASSES // WIN_PER_SIDE)
                passes_of_step.setdefault(step, []).append((b, number))

        passes_done = []
        later_sums = {}

        def project_some(mine):
            for b, number in mine:
                shared = (b == BATCH - 1 and number % 4 == 1 or b in (1, 2) and number % 6 == 3)
                project(b, number // WIN, number % WIN, shared)
                passes_done.append(number)
                if len(passes_done) == 1:
                    product(WIN_PER_SIDE)
                    normalise(WIN_PER_SIDE)
                if len(passes_done) == 3:
                    quantise_half(0, 1)
                if len(passes_done) == WIN - 2:
                    quantise_weight(1)
                if len(passes_done) == 2 * WIN - 2:
                    quantise_weight(2)
                first = WIN_PER_SIDE * (b + 2) + (0 if number < 13 else 2)
                if number in (7, 13) and b + 2 < BATCH:
                    later_sums[b] = next_acc([P, 2, HALVES, SUM_COLS])
                    sums((first, first + 1), later_sums[b], 0)
                if number - 1 in (7, 13) and b + 2 < BATCH:
                    negate_means((first, first + 1), later_sums[b], 0)

        for k in range(WIN_PER_SIDE, UNITS + WIN_PER_SIDE + 1):
            behind = WIN_PER_SIDE <= k - 1 < UNITS
            last_of_image = behind and k % WIN_PER_SIDE == 0
            mine = passes_of_step.get(k, [])
            cut = len(mine) // 2
            if behind:
                channels_to_partitions(k - 1)
            if k + 1 < UNITS:
                squares(k + 1)
            if behind:
                gain_and_shift(k - 1, low[:1], on_vector=False)
            if k + 1 < UNITS:
                root(k + 1)
            if behind:
                gain_and_shift(k - 1, low[1:] + high[:1], on_vector=False)
            if behind and k < UNITS:
                normalise(k)
            project_some(mine[:cut])
            if k + 1 < UNITS:
                reciprocal_std(k + 1)
            if behind:
                gain_and_shift(k - 1, high[1:], on_vector=True)
            if k + 2 < UNITS:
                tokens_to_partitions(k + 2)
            project_some(mine[cut : cut + 1])
            if k + 1 < UNITS:
                product(k + 1)
            project_some(mine[cut + 1 :])
            if behind:
                engine = "vector" if last_of_image else "gpsimd"
                regroup(k - 1, 0, engine)
                regroup(k - 1, 1, engine)
                if last_of_image:
                    quantise_half(k // WIN_PER_SIDE - 1, 0)
                    quantise_half(k // WIN_PER_SIDE - 1, 1)
